import numpy as np
import ml_dtypes


def mxq(x, axis, fmt="e4m3"):
    dtype, down = {"e4m3": (ml_dtypes.float8_e4m3fn, 7), "e5m2": (ml_dtypes.float8_e5m2, 14)}[fmt]
    v = np.moveaxis(np.asarray(x, np.float32).astype(ml_dtypes.bfloat16).astype(np.float64), axis, -1)
    blocks = v.reshape(v.shape[:-1] + (-1, 32))
    amax = np.abs(blocks).max(-1, keepdims=True)
    byte = np.maximum(np.where(amax > 0, np.frexp(amax)[1] - 1 + 127, 0) - down, 1)
    scale = np.exp2(byte - 127.0)
    codes = (blocks / scale).astype(np.float32).astype(dtype).astype(np.float64)
    return np.moveaxis((codes * scale).reshape(v.shape), -1, axis)


WIDE = False


def mx_kscale(k):
    if not WIDE:
        return np.ones(k)
    levels = np.array([10, -10, 5, -5, 0])
    if k % 512:
        return np.exp2(np.random.permutation(np.resize(levels, k // 32))).repeat(32)
    a = np.empty((k // 512, 16))
    for p in range(k // 512):
        a[p, :8] = np.random.permutation(np.resize(levels, 8))
        for g in range(8):
            far = levels[np.abs(levels - a[p, g]) >= 10]
            a[p, g + 8] = far[np.random.randint(len(far))]
    return np.exp2(a.ravel()).repeat(32)


BF16 = ml_dtypes.bfloat16


def bf(x):
    return np.asarray(x, np.float32).astype(BF16)


def f64(x):
    return np.asarray(x).astype(np.float64)


E2M1 = np.array([0.0, 0.5, 1.0, 1.5, 2.0, 3.0, 4.0, 6.0, -0.0, -0.5, -1.0, -1.5, -2.0, -3.0, -4.0, -6.0])


def pack_weight(w, fmt):
    k, n = w.shape
    w = f64(bf(w)).reshape(k // 32, 32, n)
    amax = np.abs(w).max(1)
    if fmt == "e4m3":
        byte = np.frexp(amax)[1] - 1 + 127 - 7
    else:
        mant, ex = np.frexp(amax / 6.0)
        byte = np.where(mant > 0.5, ex, ex - 1) + 127
    byte = np.clip(np.where(amax > 0, byte, 1), 1, 254)
    scaled = (w * np.exp2(127.0 - byte)[:, None, :]).reshape(k, n).astype(np.float32)
    by_word = np.ascontiguousarray(scaled.reshape(k // 512, 128, 4, n).transpose(0, 1, 3, 2))
    if fmt == "e4m3":
        words = by_word.astype(ml_dtypes.float8_e4m3fn).view(np.uint8)
    else:
        c = by_word.astype(ml_dtypes.float4_e2m1fn).view(np.uint8) & 0xF
        words = c[..., 0::2] | (c[..., 1::2] << 4)
    return np.ascontiguousarray(words), np.ascontiguousarray(byte.astype(np.uint8).reshape(k // 512, 16, n))


def unpack_weight(words, scales, fmt):
    g, p, n, _ = words.shape
    if fmt == "e4m3":
        vals = np.ascontiguousarray(words).view(ml_dtypes.float8_e4m3fn).astype(np.float64)
    else:
        nib = np.empty((g, p, n, 4), np.uint8)
        nib[..., 0::2] = words & 0xF
        nib[..., 1::2] = words >> 4
        vals = E2M1[nib]
    vals = vals * np.repeat(np.exp2(scales.astype(np.float64) - 127.0), 8, axis=1)[..., None]
    return vals.transpose(0, 1, 3, 2).reshape(g * 512, n)
def pack4(w):
    words, scales = pack_weight(w, "e2m1")
    return words.reshape(words.shape[0], 128, -1), scales


def unpack4(words, scales):
    return unpack_weight(words.reshape(words.shape[0], 128, -1, 2), scales, "e2m1")


B, D_IN, HID, OUT = 8192, 512, 512, 128


def draw0():
    s, t = mx_kscale(D_IN), mx_kscale(HID)
    u = np.concatenate([s, t])
    x = bf(np.random.standard_normal((B, D_IN)) * s)
    W1 = np.random.standard_normal((HID, D_IN)) / np.sqrt(D_IN) / s[None, :] * t[:, None]
    W1_words, W1_scales = pack4(W1.T)
    b1 = bf(np.random.standard_normal(HID) * 0.3 * t)
    W2 = np.random.standard_normal((OUT, D_IN + HID)) / np.sqrt(D_IN + HID) / u[None, :]
    W2_words, W2_scales = pack4(W2.T)
    b2 = bf(np.random.standard_normal(OUT) * 0.3)
    return {"x": x,
            "W1_words": W1_words,
            "W1_scales": W1_scales,
            "b1": b1,
            "W2_words": W2_words,
            "W2_scales": W2_scales,
            "b2": b2}


def core(x, W1_words, W1_scales, b1, W2_words, W2_scales, b2):
    xq = mxq(f64(x), 1, "e4m3")
    h1 = np.maximum((xq @ unpack4(W1_words, W1_scales)) + f64(b1), 0.0)
    concat = np.concatenate([xq, mxq(h1, 1, "e4m3")], axis=1)
    return (concat @ unpack4(W2_words, W2_scales)) + f64(b2)


def e4m3fn_bytes(y):
    return np.clip(np.asarray(y, np.float64), -448.0, 448.0).astype(np.float32).astype(ml_dtypes.float8_e4m3fn).view(np.uint8)


def e4m3fn_values(b):
    return np.asarray(b, np.uint8).view(ml_dtypes.float8_e4m3fn).astype(np.float64)


def setup_inputs():
    d = draw0()
    x0 = np.asarray(d['x']).astype(np.float64)
    s = (np.max(np.abs(x0), axis=(0,), keepdims=True) / 448.0).astype(np.float32)
    out = {}
    for k, v in d.items():
        if k == 'x':
            out['x_bytes'] = e4m3fn_bytes(x0 / s.astype(np.float64))
            out['x_scale'] = s
        else:
            out[k] = v
    return out


def reference(x_bytes, x_scale, W1_words, W1_scales, b1, W2_words, W2_scales, b2):
    return core(e4m3fn_values(x_bytes) * x_scale.astype(np.float64), W1_words, W1_scales, b1, W2_words, W2_scales, b2)

@@ -1,0 +1,262 @@
+from contextlib import ExitStack
+
+import concourse.mybir as mybir
+from concourse.masks import make_identity
+
+ROWS, D_IN, HID, OUT = 8192, 512, 512, 128
+FLOPS = 2 * ROWS * D_IN * HID + 2 * ROWS * (D_IN + HID) * OUT
+
+F32 = mybir.dt.float32
+BF16 = mybir.dt.bfloat16
+U32 = mybir.dt.uint32
+I32 = mybir.dt.int32
+U8 = mybir.dt.uint8
+FP8 = mybir.dt.float8_e4m3fn
+FP8X4 = mybir.dt.float8_e4m3fn_x4
+FP4X4 = mybir.dt.float4_e2m1fn_x4
+ADD = mybir.AluOpType.add
+MULT = mybir.AluOpType.mult
+RELU = mybir.ActivationFunctionType.Relu
+
+P = 128
+PACK = 4
+MAX_TILES = 4
+UNITS = [4] * 15 + [2, 2]
+N_UNITS = len(UNITS)
+VECTOR_WIDENS = {(4, 0), (9, 0)}
+VECTOR_PARTS = {N_UNITS - 1: 2, N_UNITS - 2: 2, N_UNITS - 3: 3, N_UNITS - 4: 2, N_UNITS - 5: 1}
+STARTS = [P * sum(UNITS[:c]) for c in range(N_UNITS)]
+assert P * sum(UNITS) == ROWS
+
+
+def tile_dpn_t_w4_kernel(tc, x_bytes, x_scale, W1_words, W1_scales, b1, W2_words, W2_scales, b2, out):
+    nc = tc.nc
+
+    with ExitStack() as ctx:
+        keep = ctx.enter_context(tc.tile_pool(name="keep", bufs=1))
+        work = ctx.enter_context(tc.tile_pool(name="work", bufs=3))
+        psum = ctx.enter_context(tc.psum_pool(name="psum", bufs=1))
+
+        ident = keep.tile([P, P], F32, name="ident")
+        x_scales = keep.tile([P, PACK], F32, name="x_scales")
+        w1_raw = keep.tile([P, HID * 2], U8, name="w1_raw", align_bytes=64)
+        w1 = keep.tile([P, HID * 2], U8, name="w1", align_bytes=64)
+        w1s_raw = keep.tile([P, HID], U8, name="w1s_raw", align_bytes=64)
+        w1s = keep.tile([P, HID], U8, name="w1s", align_bytes=64)
+        w2 = keep.tile([P, 2, OUT * 2], U8, name="w2", align_bytes=64)
+        w2s = keep.tile([P, 2, OUT], U8, name="w2s", align_bytes=64)
+        b1_col = keep.tile([P, PACK], BF16, name="b1_col")
+        b2_row = keep.tile([P, OUT], BF16, name="b2_row")
+        warm = keep.tile([P, 1], F32, name="warm")
+
+        x8 = {}
+
+        def load(c, lo=0, hi=MAX_TILES):
+            tiles = UNITS[c]
+            if lo == 0:
+                x8[c] = work.tile([P, MAX_TILES * D_IN], U8, name="x8", bufs=N_UNITS, align_bytes=64)
+            cols = slice(D_IN * lo, D_IN * min(hi, tiles))
+            src = x_bytes[STARTS[c] : STARTS[c] + P * tiles, :].rearrange("(p j) k -> p (j k)", j=tiles)
+            nc.sync.dma_start(out=x8[c][:, cols], in_=src[:, cols])
+
+        nc.vector.memset(w1s_raw[:].bitcast(U32), 0)
+        nc.vector.memset(w2s[:].rearrange("p g n -> p (g n)").bitcast(U32), 0)
+        nc.vector.memset(warm[:], 0.0)
+        nc.scalar.dma_start(out=x_scales[:], in_=x_scale.rearrange("o (p t) -> p (o t)", t=PACK))
+        load(0, 0, 2)
+        nc.sync.dma_start(out=w1_raw[:], in_=W1_words[0])
+        for q in range(4):
+            nc.sync.dma_start(
+                out=w1s_raw[32 * q : 32 * q + 4, :].bitcast(I32), in_=W1_scales[0, 4 * q : 4 * q + 4, :].bitcast(I32)
+            )
+        load(0, 2, 4)
+        nc.scalar.dma_start(out=b1_col[:], in_=b1.rearrange("(p t) -> p t", t=PACK))
+        nc.scalar.activation(out=warm[:], in_=warm[:], func=RELU)
+        make_identity(nc, ident[:])
+        load(1)
+        load(2)
+        nc.sync.dma_start(out=w2[:], in_=W2_words.rearrange("g p n -> p g n"))
+        for q in range(4):
+            nc.sync.dma_start(
+                out=w2s[32 * q : 32 * q + 4, :, :].bitcast(I32),
+                in_=W2_scales.bitcast(I32)[:, 4 * q : 4 * q + 4, :].rearrange("g q n -> q g n"),
+            )
+        nc.sync.dma_start(out=b2_row[:], in_=b2.partition_broadcast(P))
+        for c in range(3, N_UNITS):
+            load(c)
+
+        def permute_weights():
+            nc.vector.tensor_copy(
+                out=w1[:].rearrange("p (t m b) -> p t m b", t=PACK, b=2),
+                in_=w1_raw[:].rearrange("p (m t b) -> p t m b", t=PACK, b=2),
+            )
+            nc.vector.tensor_copy(
+                out=w1s[:].rearrange("p (t m) -> p t m", t=PACK),
+                in_=w1s_raw[:].rearrange("p (m t) -> p t m", t=PACK),
+            )
+
+        xb, xt, xg, xq, xs = {}, {}, {}, {}, {}
+        h, hs, hg, hq, hsc = {}, {}, {}, {}, {}
+        acc, ob = {}, {}
+
+        def live(c, half=0):
+            return 0 <= c < N_UNITS and 2 * half < UNITS[c]
+
+        def widen_x(c, lo=0, hi=MAX_TILES):
+            if not live(c):
+                return
+            if lo == 0:
+                xb[c] = work.tile([P, MAX_TILES * D_IN], BF16, name="xb", bufs=4, align_bytes=64)
+            cols = slice(D_IN * lo, D_IN * min(hi, UNITS[c]))
+            copy = nc.vector.tensor_copy if (c, lo) in VECTOR_WIDENS else nc.scalar.copy
+            copy(out=xb[c][:, cols], in_=x8[c][:, cols].bitcast(FP8))
+
+        def transpose_x(c, half):
+            if not live(c, half):
+                return
+            words = xb[c][:].bitcast(F32)
+            xt[c, half] = psum.tile([P, 2, 2, P], F32, name="xt", bufs=2)
+            for j in range(2):
+                w0 = (2 * half + j) * (D_IN // 2)
+                for u in range(2):
+                    nc.tensor.transpose(xt[c, half][:, u, j, :], words[:, w0 + u : w0 + D_IN // 2 : 2], ident[:])
+
+        def scale_x(c, half):
+            if not live(c, half):
+                return
+            if half == 0:
+                xg[c] = work.tile([P, MAX_TILES * D_IN], BF16, name="xg", align_bytes=64)
+            nc.vector.tensor_tensor(
+                out=xg[c][:, 2 * D_IN * half : 2 * D_IN * (half + 1)].rearrange("p (n u e) -> p n u e", u=2, e=2),
+                in0=xt[c, half][:]
+                .rearrange("p u j n -> p (u j n)")
+                .bitcast(BF16)
+                .rearrange("p (u n e) -> p n u e", u=2, e=2),
+                in1=x_scales[:].rearrange("p (u e) -> p u e", e=2).unsqueeze(1).to_broadcast([P, 2 * P, 2, 2]),
+                op=MULT,
+            )
+
+        def quantize_x(c):
+            if not live(c):
+                return
+            n = P * UNITS[c]
+            xq[c] = work.tile([P, MAX_TILES * P], U32, name="xq", bufs=5, align_bytes=64)
+            xs[c] = work.tile([P, MAX_TILES * P], U8, name="xs", bufs=5, align_bytes=64)
+            nc.vector.quantize_mx(
+                out=xq[c][:, :n].bitcast(FP8X4), scales=xs[c][:, :n], in_=xg[c][:, : PACK * n]
+            )
+
+        def layer1(c, t):
+            if not live(c):
+                return
+            n = P * UNITS[c]
+            h[c, t] = psum.tile([P, MAX_TILES * P], F32, name="h%d" % t)
+            nc.tensor.matmul_mx(
+                out=h[c, t][:, :n],
+                lhsT=w1[:, 2 * P * t : 2 * P * (t + 1)].bitcast(FP4X4),
+                lhsT_scale=w1s[:, P * t : P * (t + 1)],
+                rhs=xq[c][:, :n].bitcast(FP8X4),
+                rhs_scale=xs[c][:, :n],
+                start=True,
+                stop=True,
+            )
+
+        def relu(c, t):
+            if not live(c):
+                return
+            n = P * UNITS[c]
+            if c not in hs:
+                hs[c] = work.tile([P, PACK, MAX_TILES * P], BF16, name="hs", align_bytes=64)
+            dst = hs[c][:, t, :n]
+            nc.scalar.activation(out=dst, in_=h[c, t][:, :n], func=RELU, bias=b1_col[:, t : t + 1])
+
+        def interleave_h(c, on_vector=False):
+            if not live(c):
+                return
+            if c not in hg:
+                hg[c] = work.tile([P, MAX_TILES * P, PACK], BF16, name="hg", align_bytes=64)
+            for j in range(UNITS[c]):
+                if on_vector != (j < VECTOR_PARTS.get(c, 0)):
+                    continue
+                rows = slice(P * j, P * (j + 1))
+                src = hs[c][:, :, rows].rearrange("p t n -> p n t")
+                if on_vector:
+                    nc.vector.tensor_copy(out=hg[c][:, rows, :], in_=src)
+                else:
+                    nc.gpsimd.tensor_scalar(
+                        out=hg[c][:, rows, :], in0=src, scalar1=1.0, scalar2=0.0, op0=MULT, op1=ADD
+                    )
+
+        def quantize_h(c):
+            if not live(c):
+                return
+            n = P * UNITS[c]
+            hq[c] = work.tile([P, MAX_TILES * P], U32, name="hq", align_bytes=64)
+            hsc[c] = work.tile([P, MAX_TILES * P], U8, name="hsc", align_bytes=64)
+            nc.vector.quantize_mx(
+                out=hq[c][:, :n].bitcast(FP8X4), scales=hsc[c][:, :n], in_=hg[c][:, :n, :].rearrange("p n t -> p (n t)")
+            )
+
+        def layer2(c):
+            if not live(c):
+                return
+            acc[c] = psum.tile([P, MAX_TILES, OUT], F32, name="acc", bufs=2)
+            for j in range(UNITS[c]):
+                cols = slice(P * j, P * (j + 1))
+                for g, codes, scales in ((0, xq[c], xs[c]), (1, hq[c], hsc[c])):
+                    nc.tensor.matmul_mx(
+                        out=acc[c][:, j, :],
+                        lhsT=codes[:, cols].bitcast(FP8X4),
+                        lhsT_scale=scales[:, cols],
+                        rhs=w2[:, g, :].bitcast(FP4X4),
+                        rhs_scale=w2s[:, g, :],
+                        start=(g == 0),
+                        stop=(g == 1),
+                    )
+
+        def add_b2(c):
+            if not live(c):
+                return
+            tiles = UNITS[c]
+            ob[c] = work.tile([P, MAX_TILES, OUT], F32, name="ob")
+            nc.vector.tensor_tensor(
+                out=ob[c][:, :tiles, :],
+                in0=acc[c][:, :tiles, :],
+                in1=b2_row[:].unsqueeze(1).to_broadcast([P, tiles, OUT]),
+                op=ADD,
+            )
+
+        def store(c):
+            if not live(c):
+                return
+            tiles = UNITS[c]
+            nc.sync.dma_start(
+                out=out[STARTS[c] : STARTS[c] + P * tiles, :].rearrange("(p j) o -> p (j o)", j=tiles),
+                in_=ob[c][:, :tiles, :].rearrange("p j o -> p (j o)"),
+            )
+
+        with tc.manual_schedule():
+            widen_x(0, 0, 2)
+            permute_weights()
+            widen_x(0, 2, 4)
+            for s in range(-5, N_UNITS):
+                for t in range(PACK):
+                    relu(s + 2, t)
+                widen_x(s + 6)
+                if s == -5:
+                    transpose_x(0, 0)
+                    transpose_x(0, 1)
+                quantize_h(s)
+                interleave_h(s + 1)
+                layer2(s)
+                scale_x(s + 4, 0)
+                scale_x(s + 4, 1)
+                for t in range(PACK):
+                    layer1(s + 3, t)
+                interleave_h(s + 1, on_vector=True)
+                add_b2(s)
+                quantize_x(s + 4)
+                if s > -5:
+                    transpose_x(s + 5, 0)
+                    transpose_x(s + 5, 1)
+                store(s)

@@ -17,14 +17,16 @@ FP4X4 = mybir.dt.float4_e2m1fn_x4
 ADD = mybir.AluOpType.add
 MULT = mybir.AluOpType.mult
 RELU = mybir.ActivationFunctionType.Relu
+COPY = mybir.ActivationFunctionType.Copy
 
 P = 128
 PACK = 4
 MAX_TILES = 4
-UNITS = [4] * 15 + [2, 2]
+UNITS = [2, 2] + [4] * 14 + [2, 2]
 N_UNITS = len(UNITS)
-VECTOR_WIDENS = {(4, 0), (9, 0)}
-VECTOR_PARTS = {N_UNITS - 1: 2, N_UNITS - 2: 2, N_UNITS - 3: 3, N_UNITS - 4: 2, N_UNITS - 5: 1}
+VECTOR_WIDENS = {0}
+GPSIMD_EIGHTHS = 7
+TAIL_UNITS = 2
 STARTS = [P * sum(UNITS[:c]) for c in range(N_UNITS)]
 assert P * sum(UNITS) == ROWS
 
@@ -36,6 +38,7 @@ def tile_dpn_t_w4_kernel(tc, x_bytes, x_scale, W1_words, W1_scales, b1, W2_words
         keep = ctx.enter_context(tc.tile_pool(name="keep", bufs=1))
         work = ctx.enter_context(tc.tile_pool(name="work", bufs=3))
         psum = ctx.enter_context(tc.psum_pool(name="psum", bufs=1))
+        ctx.enter_context(tc.manual_schedule())
 
         ident = keep.tile([P, P], F32, name="ident")
         x_scales = keep.tile([P, PACK], F32, name="x_scales")
@@ -47,34 +50,29 @@ def tile_dpn_t_w4_kernel(tc, x_bytes, x_scale, W1_words, W1_scales, b1, W2_words
         w2s = keep.tile([P, 2, OUT], U8, name="w2s", align_bytes=64)
         b1_col = keep.tile([P, PACK], BF16, name="b1_col")
         b2_row = keep.tile([P, OUT], BF16, name="b2_row")
-        warm = keep.tile([P, 1], F32, name="warm")
 
         x8 = {}
 
-        def load(c, lo=0, hi=MAX_TILES):
+        def load(c):
             tiles = UNITS[c]
-            if lo == 0:
-                x8[c] = work.tile([P, MAX_TILES * D_IN], U8, name="x8", bufs=N_UNITS, align_bytes=64)
-            cols = slice(D_IN * lo, D_IN * min(hi, tiles))
+            x8[c] = work.tile([P, MAX_TILES * D_IN], U8, name="x8", bufs=N_UNITS, align_bytes=64)
             src = x_bytes[STARTS[c] : STARTS[c] + P * tiles, :].rearrange("(p j) k -> p (j k)", j=tiles)
-            nc.sync.dma_start(out=x8[c][:, cols], in_=src[:, cols])
+            nc.sync.dma_start(out=x8[c][:, : D_IN * tiles], in_=src)
 
         nc.vector.memset(w1s_raw[:].bitcast(U32), 0)
         nc.vector.memset(w2s[:].rearrange("p g n -> p (g n)").bitcast(U32), 0)
-        nc.vector.memset(warm[:], 0.0)
+        load(0)
+        load(1)
         nc.scalar.dma_start(out=x_scales[:], in_=x_scale.rearrange("o (p t) -> p (o t)", t=PACK))
-        load(0, 0, 2)
         nc.sync.dma_start(out=w1_raw[:], in_=W1_words[0])
         for q in range(4):
             nc.sync.dma_start(
                 out=w1s_raw[32 * q : 32 * q + 4, :].bitcast(I32), in_=W1_scales[0, 4 * q : 4 * q + 4, :].bitcast(I32)
             )
-        load(0, 2, 4)
-        nc.scalar.dma_start(out=b1_col[:], in_=b1.rearrange("(p t) -> p t", t=PACK))
-        nc.scalar.activation(out=warm[:], in_=warm[:], func=RELU)
         make_identity(nc, ident[:])
-        load(1)
         load(2)
+        nc.sync.dma_start(out=b1_col[:], in_=b1.rearrange("(p t) -> p t", t=PACK))
+        load(3)
         nc.sync.dma_start(out=w2[:], in_=W2_words.rearrange("g p n -> p g n"))
         for q in range(4):
             nc.sync.dma_start(
@@ -82,7 +80,7 @@ def tile_dpn_t_w4_kernel(tc, x_bytes, x_scale, W1_words, W1_scales, b1, W2_words
                 in_=W2_scales.bitcast(I32)[:, 4 * q : 4 * q + 4, :].rearrange("g q n -> q g n"),
             )
         nc.sync.dma_start(out=b2_row[:], in_=b2.partition_broadcast(P))
-        for c in range(3, N_UNITS):
+        for c in range(4, N_UNITS):
             load(c)
 
         def permute_weights():
@@ -102,21 +100,25 @@ def tile_dpn_t_w4_kernel(tc, x_bytes, x_scale, W1_words, W1_scales, b1, W2_words
         def live(c, half=0):
             return 0 <= c < N_UNITS and 2 * half < UNITS[c]
 
-        def widen_x(c, lo=0, hi=MAX_TILES):
+        def widen_x(c):
             if not live(c):
                 return
-            if lo == 0:
-                xb[c] = work.tile([P, MAX_TILES * D_IN], BF16, name="xb", bufs=4, align_bytes=64)
-            cols = slice(D_IN * lo, D_IN * min(hi, UNITS[c]))
-            copy = nc.vector.tensor_copy if (c, lo) in VECTOR_WIDENS else nc.scalar.copy
-            copy(out=xb[c][:, cols], in_=x8[c][:, cols].bitcast(FP8))
+            xb[c] = work.tile([P, MAX_TILES * D_IN], BF16, name="xb", bufs=4, align_bytes=64)
+            cols = slice(0, D_IN * UNITS[c])
+            src = x8[c][:, cols].bitcast(FP8)
+            if c in VECTOR_WIDENS:
+                nc.vector.tensor_copy(out=xb[c][:, cols], in_=src)
+            elif c == 1:
+                nc.scalar.activation(out=xb[c][:, cols], in_=src, func=COPY)
+            else:
+                nc.scalar.copy(out=xb[c][:, cols], in_=src)
 
         def transpose_x(c, half):
             if not live(c, half):
                 return
             words = xb[c][:].bitcast(F32)
             xt[c, half] = psum.tile([P, 2, 2, P], F32, name="xt", bufs=2)
-            for j in range(2):
+            for j in range(min(2, UNITS[c] - 2 * half)):
                 w0 = (2 * half + j) * (D_IN // 2)
                 for u in range(2):
                     nc.tensor.transpose(xt[c, half][:, u, j, :], words[:, w0 + u : w0 + D_IN // 2 : 2], ident[:])
@@ -125,14 +127,16 @@ def tile_dpn_t_w4_kernel(tc, x_bytes, x_scale, W1_words, W1_scales, b1, W2_words
             if not live(c, half):
                 return
             if half == 0:
-                xg[c] = work.tile([P, MAX_TILES * D_IN], BF16, name="xg", align_bytes=64)
+                xg[c] = work.tile([P, MAX_TILES * D_IN], BF16, name="xg", bufs=2, align_bytes=64)
+            n = P * min(2, UNITS[c] - 2 * half)
+            c0 = 2 * D_IN * half
             nc.vector.tensor_tensor(
-                out=xg[c][:, 2 * D_IN * half : 2 * D_IN * (half + 1)].rearrange("p (n u e) -> p n u e", u=2, e=2),
+                out=xg[c][:, c0 : c0 + PACK * n].rearrange("p (n u e) -> p n u e", u=2, e=2),
                 in0=xt[c, half][:]
                 .rearrange("p u j n -> p (u j n)")
                 .bitcast(BF16)
-                .rearrange("p (u n e) -> p n u e", u=2, e=2),
-                in1=x_scales[:].rearrange("p (u e) -> p u e", e=2).unsqueeze(1).to_broadcast([P, 2 * P, 2, 2]),
+                .rearrange("p (u n e) -> p n u e", u=2, e=2)[:, :n],
+                in1=x_scales[:].rearrange("p (u e) -> p u e", e=2).unsqueeze(1).to_broadcast([P, n, 2, 2]),
                 op=MULT,
             )
 
@@ -140,8 +144,8 @@ def tile_dpn_t_w4_kernel(tc, x_bytes, x_scale, W1_words, W1_scales, b1, W2_words
             if not live(c):
                 return
             n = P * UNITS[c]
-            xq[c] = work.tile([P, MAX_TILES * P], U32, name="xq", bufs=5, align_bytes=64)
-            xs[c] = work.tile([P, MAX_TILES * P], U8, name="xs", bufs=5, align_bytes=64)
+            xq[c] = work.tile([P, MAX_TILES * P], U32, name="xq", bufs=6, align_bytes=64)
+            xs[c] = work.tile([P, MAX_TILES * P], U8, name="xs", bufs=6, align_bytes=64)
             nc.vector.quantize_mx(
                 out=xq[c][:, :n].bitcast(FP8X4), scales=xs[c][:, :n], in_=xg[c][:, : PACK * n]
             )
@@ -170,22 +174,21 @@ def tile_dpn_t_w4_kernel(tc, x_bytes, x_scale, W1_words, W1_scales, b1, W2_words
             dst = hs[c][:, t, :n]
             nc.scalar.activation(out=dst, in_=h[c, t][:, :n], func=RELU, bias=b1_col[:, t : t + 1])
 
-        def interleave_h(c, on_vector=False):
+        def interleave_h(c, on_vector):
             if not live(c):
                 return
+            n = P * UNITS[c]
+            cut = 0 if c >= N_UNITS - TAIL_UNITS else n * GPSIMD_EIGHTHS // 8
             if c not in hg:
-                hg[c] = work.tile([P, MAX_TILES * P, PACK], BF16, name="hg", align_bytes=64)
-            for j in range(UNITS[c]):
-                if on_vector != (j < VECTOR_PARTS.get(c, 0)):
-                    continue
-                rows = slice(P * j, P * (j + 1))
-                src = hs[c][:, :, rows].rearrange("p t n -> p n t")
-                if on_vector:
-                    nc.vector.tensor_copy(out=hg[c][:, rows, :], in_=src)
-                else:
-                    nc.gpsimd.tensor_scalar(
-                        out=hg[c][:, rows, :], in0=src, scalar1=1.0, scalar2=0.0, op0=MULT, op1=ADD
-                    )
+                hg[c] = work.tile([P, MAX_TILES * P, PACK], BF16, name="hg", bufs=1, align_bytes=64)
+            rows = slice(cut, n) if on_vector else slice(0, cut)
+            if rows.start == rows.stop:
+                return
+            src = hs[c][:, :, rows].rearrange("p t n -> p n t")
+            if on_vector:
+                nc.vector.tensor_copy(out=hg[c][:, rows, :], in_=src)
+            else:
+                nc.gpsimd.tensor_scalar(out=hg[c][:, rows, :], in0=src, scalar1=1.0, scalar2=0.0, op0=MULT, op1=ADD)
 
         def quantize_h(c):
             if not live(c):
@@ -235,28 +238,24 @@ def tile_dpn_t_w4_kernel(tc, x_bytes, x_scale, W1_words, W1_scales, b1, W2_words
                 in_=ob[c][:, :tiles, :].rearrange("p j o -> p (j o)"),
             )
 
-        with tc.manual_schedule():
-            widen_x(0, 0, 2)
-            permute_weights()
-            widen_x(0, 2, 4)
-            for s in range(-5, N_UNITS):
-                for t in range(PACK):
-                    relu(s + 2, t)
-                widen_x(s + 6)
-                if s == -5:
-                    transpose_x(0, 0)
-                    transpose_x(0, 1)
-                quantize_h(s)
-                interleave_h(s + 1)
-                layer2(s)
-                scale_x(s + 4, 0)
-                scale_x(s + 4, 1)
-                for t in range(PACK):
-                    layer1(s + 3, t)
-                interleave_h(s + 1, on_vector=True)
-                add_b2(s)
-                quantize_x(s + 4)
-                if s > -5:
-                    transpose_x(s + 5, 0)
-                    transpose_x(s + 5, 1)
-                store(s)
+        widen_x(0)
+        widen_x(1)
+        transpose_x(0, 0)
+        transpose_x(0, 1)
+        permute_weights()
+        for s in range(N_UNITS + 4):
+            for t in range(PACK):
+                layer1(s - 1, t)
+                relu(s - 1, t)
+            widen_x(s + 2)
+            interleave_h(s - 2, on_vector=False)
+            scale_x(s, 0)
+            transpose_x(s + 1, 0)
+            layer2(s - 3)
+            scale_x(s, 1)
+            transpose_x(s + 1, 1)
+            add_b2(s - 4)
+            store(s - 4)
+            interleave_h(s - 2, on_vector=True)
+            quantize_x(s)
+            quantize_h(s - 2)

@@ -21,14 +21,22 @@ COPY = mybir.ActivationFunctionType.Copy
 
 P = 128
 PACK = 4
+TILES = ROWS // P
 MAX_TILES = 4
 UNITS = [2, 2] + [4] * 14 + [2, 2]
 N_UNITS = len(UNITS)
-VECTOR_WIDENS = {0}
-GPSIMD_EIGHTHS = 7
-TAIL_UNITS = 2
-STARTS = [P * sum(UNITS[:c]) for c in range(N_UNITS)]
-assert P * sum(UNITS) == ROWS
+FIRST = [sum(UNITS[:c]) for c in range(N_UNITS + 1)]
+LOADS = [4, 4, 4, 4] + [8] * 6
+XT_BANKS = 2
+ACC_BANKS = 2
+OUT_LAG = 4
+GPSIMD_TENTHS = 8
+SCALAR_EIGHTHS = 3
+SCALAR_HEAD = 10
+VECTOR_HEAD = [0, 4, 4, 4]
+STREAM_START = SCALAR_HEAD + sum(VECTOR_HEAD)
+STREAM_QUARTERS = 12
+assert FIRST[-1] == TILES and sum(LOADS) == TILES
 
 
 def tile_dpn_t_w4_kernel(tc, x_bytes, x_scale, W1_words, W1_scales, b1, W2_words, W2_scales, b2, out):
@@ -50,19 +58,19 @@ def tile_dpn_t_w4_kernel(tc, x_bytes, x_scale, W1_words, W1_scales, b1, W2_words
         w2s = keep.tile([P, 2, OUT], U8, name="w2s", align_bytes=64)
         b1_col = keep.tile([P, PACK], BF16, name="b1_col")
         b2_row = keep.tile([P, OUT], BF16, name="b2_row")
+        x8 = keep.tile([P, TILES * D_IN], U8, name="x8", align_bytes=64)
+        xb = keep.tile([P, TILES * D_IN], BF16, name="xb", align_bytes=64)
 
-        x8 = {}
+        x_rows = x_bytes.rearrange("(p j) k -> p (j k)", j=TILES)
+        out_rows = out.rearrange("(p j) o -> p (j o)", j=TILES)
 
-        def load(c):
-            tiles = UNITS[c]
-            x8[c] = work.tile([P, MAX_TILES * D_IN], U8, name="x8", bufs=N_UNITS, align_bytes=64)
-            src = x_bytes[STARTS[c] : STARTS[c] + P * tiles, :].rearrange("(p j) k -> p (j k)", j=tiles)
-            nc.sync.dma_start(out=x8[c][:, : D_IN * tiles], in_=src)
+        def load(i):
+            cols = slice(D_IN * sum(LOADS[:i]), D_IN * sum(LOADS[: i + 1]))
+            nc.sync.dma_start(out=x8[:, cols], in_=x_rows[:, cols])
 
         nc.vector.memset(w1s_raw[:].bitcast(U32), 0)
         nc.vector.memset(w2s[:].rearrange("p g n -> p (g n)").bitcast(U32), 0)
         load(0)
-        load(1)
         nc.scalar.dma_start(out=x_scales[:], in_=x_scale.rearrange("o (p t) -> p (o t)", t=PACK))
         nc.sync.dma_start(out=w1_raw[:], in_=W1_words[0])
         for q in range(4):
@@ -70,9 +78,11 @@ def tile_dpn_t_w4_kernel(tc, x_bytes, x_scale, W1_words, W1_scales, b1, W2_words
                 out=w1s_raw[32 * q : 32 * q + 4, :].bitcast(I32), in_=W1_scales[0, 4 * q : 4 * q + 4, :].bitcast(I32)
             )
         make_identity(nc, ident[:])
+        load(1)
         load(2)
         nc.sync.dma_start(out=b1_col[:], in_=b1.rearrange("(p t) -> p t", t=PACK))
         load(3)
+        load(4)
         nc.sync.dma_start(out=w2[:], in_=W2_words.rearrange("g p n -> p g n"))
         for q in range(4):
             nc.sync.dma_start(
@@ -80,8 +90,8 @@ def tile_dpn_t_w4_kernel(tc, x_bytes, x_scale, W1_words, W1_scales, b1, W2_words
                 in_=W2_scales.bitcast(I32)[:, 4 * q : 4 * q + 4, :].rearrange("g q n -> q g n"),
             )
         nc.sync.dma_start(out=b2_row[:], in_=b2.partition_broadcast(P))
-        for c in range(4, N_UNITS):
-            load(c)
+        for i in range(5, len(LOADS)):
+            load(i)
 
         def permute_weights():
             nc.vector.tensor_copy(
@@ -93,57 +103,60 @@ def tile_dpn_t_w4_kernel(tc, x_bytes, x_scale, W1_words, W1_scales, b1, W2_words
                 in_=w1s_raw[:].rearrange("p (m t) -> p t m", t=PACK),
             )
 
-        xb, xt, xg, xq, xs = {}, {}, {}, {}, {}
+        xt, xg, xq, xs = {}, {}, {}, {}
         h, hs, hg, hq, hsc = {}, {}, {}, {}, {}
         acc, ob = {}, {}
 
-        def live(c, half=0):
-            return 0 <= c < N_UNITS and 2 * half < UNITS[c]
+        def live(c):
+            return 0 <= c < N_UNITS
 
-        def widen_x(c):
-            if not live(c):
-                return
-            xb[c] = work.tile([P, MAX_TILES * D_IN], BF16, name="xb", bufs=4, align_bytes=64)
-            cols = slice(0, D_IN * UNITS[c])
-            src = x8[c][:, cols].bitcast(FP8)
-            if c in VECTOR_WIDENS:
-                nc.vector.tensor_copy(out=xb[c][:, cols], in_=src)
-            elif c == 1:
-                nc.scalar.activation(out=xb[c][:, cols], in_=src, func=COPY)
-            else:
-                nc.scalar.copy(out=xb[c][:, cols], in_=src)
+        def rows_of(c):
+            return P * UNITS[c] if live(c) else 0
 
-        def transpose_x(c, half):
-            if not live(c, half):
+        groups = [(c, j) for c in range(N_UNITS) for j in range(0, UNITS[c], 2)]
+
+        def widen(lo, hi, copy):
+            cols = slice(lo, min(hi, TILES * D_IN))
+            if cols.start < cols.stop:
+                copy(out=xb[:, cols], in_=x8[:, cols].bitcast(FP8))
+
+        def copy_by_activation(out, in_):
+            nc.scalar.activation(out=out, in_=in_, func=COPY)
+
+        def transpose_x(g):
+            if g >= len(groups):
                 return
-            words = xb[c][:].bitcast(F32)
-            xt[c, half] = psum.tile([P, 2, 2, P], F32, name="xt", bufs=2)
-            for j in range(min(2, UNITS[c] - 2 * half)):
-                w0 = (2 * half + j) * (D_IN // 2)
+            c, j0 = groups[g]
+            words = xb[:].bitcast(F32)
+            xt[g] = psum.tile([P, 2, 2, P], F32, name="xt", bufs=XT_BANKS)
+            for j in range(min(2, UNITS[c] - j0)):
+                w0 = (FIRST[c] + j0 + j) * (D_IN // 2)
                 for u in range(2):
-                    nc.tensor.transpose(xt[c, half][:, u, j, :], words[:, w0 + u : w0 + D_IN // 2 : 2], ident[:])
+                    nc.tensor.transpose(xt[g][:, u, j, :], words[:, w0 + u : w0 + D_IN // 2 : 2], ident[:])
 
-        def scale_x(c, half):
-            if not live(c, half):
+        def scale_x(c, j0):
+            if (c, j0) not in groups:
                 return
-            if half == 0:
+            g = groups.index((c, j0))
+            if j0 == 0:
                 xg[c] = work.tile([P, MAX_TILES * D_IN], BF16, name="xg", bufs=2, align_bytes=64)
-            n = P * min(2, UNITS[c] - 2 * half)
-            c0 = 2 * D_IN * half
+            n = P * min(2, UNITS[c] - j0)
+            c0 = D_IN * j0
             nc.vector.tensor_tensor(
                 out=xg[c][:, c0 : c0 + PACK * n].rearrange("p (n u e) -> p n u e", u=2, e=2),
-                in0=xt[c, half][:]
+                in0=xt[g][:]
                 .rearrange("p u j n -> p (u j n)")
                 .bitcast(BF16)
                 .rearrange("p (u n e) -> p n u e", u=2, e=2)[:, :n],
                 in1=x_scales[:].rearrange("p (u e) -> p u e", e=2).unsqueeze(1).to_broadcast([P, n, 2, 2]),
                 op=MULT,
             )
+            transpose_x(g + XT_BANKS)
 
         def quantize_x(c):
             if not live(c):
                 return
-            n = P * UNITS[c]
+            n = rows_of(c)
             xq[c] = work.tile([P, MAX_TILES * P], U32, name="xq", bufs=6, align_bytes=64)
             xs[c] = work.tile([P, MAX_TILES * P], U8, name="xs", bufs=6, align_bytes=64)
             nc.vector.quantize_mx(
@@ -153,7 +166,7 @@ def tile_dpn_t_w4_kernel(tc, x_bytes, x_scale, W1_words, W1_scales, b1, W2_words
         def layer1(c, t):
             if not live(c):
                 return
-            n = P * UNITS[c]
+            n = rows_of(c)
             h[c, t] = psum.tile([P, MAX_TILES * P], F32, name="h%d" % t)
             nc.tensor.matmul_mx(
                 out=h[c, t][:, :n],
@@ -168,32 +181,38 @@ def tile_dpn_t_w4_kernel(tc, x_bytes, x_scale, W1_words, W1_scales, b1, W2_words
         def relu(c, t):
             if not live(c):
                 return
-            n = P * UNITS[c]
+            n = rows_of(c)
             if c not in hs:
                 hs[c] = work.tile([P, PACK, MAX_TILES * P], BF16, name="hs", align_bytes=64)
             dst = hs[c][:, t, :n]
             nc.scalar.activation(out=dst, in_=h[c, t][:, :n], func=RELU, bias=b1_col[:, t : t + 1])
 
-        def interleave_h(c, on_vector):
+        def interleave_h(c, engine):
             if not live(c):
                 return
-            n = P * UNITS[c]
-            cut = 0 if c >= N_UNITS - TAIL_UNITS else n * GPSIMD_EIGHTHS // 8
+            n = rows_of(c)
+            beside = PACK * rows_of(c + 2) + rows_of(c + 2 - OUT_LAG)
+            cut0 = min(n, beside * GPSIMD_TENTHS // 10 // PACK // 16 * 16) if live(c + 2) else 0
+            cut1 = cut0 + ((n - cut0) * SCALAR_EIGHTHS // 8 // 16 * 16 if not live(c + 3) else 0)
             if c not in hg:
                 hg[c] = work.tile([P, MAX_TILES * P, PACK], BF16, name="hg", bufs=1, align_bytes=64)
-            rows = slice(cut, n) if on_vector else slice(0, cut)
+            rows = {"gpsimd": slice(0, cut0), "scalar": slice(cut0, cut1), "vector": slice(cut1, n)}[engine]
             if rows.start == rows.stop:
                 return
-            src = hs[c][:, :, rows].rearrange("p t n -> p n t")
-            if on_vector:
-                nc.vector.tensor_copy(out=hg[c][:, rows, :], in_=src)
+            run = 2 if engine == "gpsimd" else PACK
+            src = hs[c][:, :, rows].rearrange("p t (n i) -> p n t i", i=run)
+            dst = hg[c][:, rows, :].rearrange("p (n i) t -> p n t i", i=run)
+            if engine == "vector":
+                nc.vector.tensor_copy(out=dst, in_=src)
+            elif engine == "scalar":
+                nc.scalar.copy(out=dst, in_=src)
             else:
-                nc.gpsimd.tensor_scalar(out=hg[c][:, rows, :], in0=src, scalar1=1.0, scalar2=0.0, op0=MULT, op1=ADD)
+                nc.gpsimd.tensor_scalar(out=dst, in0=src, scalar1=1.0, scalar2=0.0, op0=MULT, op1=ADD)
 
         def quantize_h(c):
             if not live(c):
                 return
-            n = P * UNITS[c]
+            n = rows_of(c)
             hq[c] = work.tile([P, MAX_TILES * P], U32, name="hq", align_bytes=64)
             hsc[c] = work.tile([P, MAX_TILES * P], U8, name="hsc", align_bytes=64)
             nc.vector.quantize_mx(
@@ -203,7 +222,7 @@ def tile_dpn_t_w4_kernel(tc, x_bytes, x_scale, W1_words, W1_scales, b1, W2_words
         def layer2(c):
             if not live(c):
                 return
-            acc[c] = psum.tile([P, MAX_TILES, OUT], F32, name="acc", bufs=2)
+            acc[c] = psum.tile([P, MAX_TILES, OUT], F32, name="acc", bufs=ACC_BANKS)
             for j in range(UNITS[c]):
                 cols = slice(P * j, P * (j + 1))
                 for g, codes, scales in ((0, xq[c], xs[c]), (1, hq[c], hsc[c])):
@@ -217,7 +236,7 @@ def tile_dpn_t_w4_kernel(tc, x_bytes, x_scale, W1_words, W1_scales, b1, W2_words
                         stop=(g == 1),
                     )
 
-        def add_b2(c):
+        def add_b2_and_store(c):
             if not live(c):
                 return
             tiles = UNITS[c]
@@ -228,34 +247,33 @@ def tile_dpn_t_w4_kernel(tc, x_bytes, x_scale, W1_words, W1_scales, b1, W2_words
                 in1=b2_row[:].unsqueeze(1).to_broadcast([P, tiles, OUT]),
                 op=ADD,
             )
-
-        def store(c):
-            if not live(c):
-                return
-            tiles = UNITS[c]
             nc.sync.dma_start(
-                out=out[STARTS[c] : STARTS[c] + P * tiles, :].rearrange("(p j) o -> p (j o)", j=tiles),
+                out=out_rows[:, OUT * FIRST[c] : OUT * FIRST[c + 1]],
                 in_=ob[c][:, :tiles, :].rearrange("p j o -> p (j o)"),
             )
 
-        widen_x(0)
-        widen_x(1)
-        transpose_x(0, 0)
-        transpose_x(0, 1)
+        def stream_col(s):
+            return D_IN * STREAM_START + D_IN * STREAM_QUARTERS * max(0, s - 1) // 4
+
+        widen(0, 2 * D_IN, nc.vector.tensor_copy)
+        widen(2 * D_IN, 4 * D_IN, copy_by_activation)
+        widen(4 * D_IN, 8 * D_IN, nc.scalar.copy)
+        widen(8 * D_IN, SCALAR_HEAD * D_IN, nc.scalar.copy)
+        for g in range(XT_BANKS):
+            transpose_x(g)
         permute_weights()
-        for s in range(N_UNITS + 4):
+        for s in range(N_UNITS + OUT_LAG):
+            interleave_h(s - 2, "scalar")
             for t in range(PACK):
                 layer1(s - 1, t)
                 relu(s - 1, t)
-            widen_x(s + 2)
-            interleave_h(s - 2, on_vector=False)
+            widen(stream_col(s), stream_col(s + 1), nc.scalar.copy)
+            interleave_h(s - 2, "gpsimd")
             scale_x(s, 0)
-            transpose_x(s + 1, 0)
             layer2(s - 3)
-            scale_x(s, 1)
-            transpose_x(s + 1, 1)
-            add_b2(s - 4)
-            store(s - 4)
-            interleave_h(s - 2, on_vector=True)
+            scale_x(s, 2)
+            add_b2_and_store(s - OUT_LAG)
+            interleave_h(s - 2, "vector")
+            widen((SCALAR_HEAD + sum(VECTOR_HEAD[:s])) * D_IN, (SCALAR_HEAD + sum(VECTOR_HEAD[: s + 1])) * D_IN, nc.vector.tensor_copy)
             quantize_x(s)
             quantize_h(s - 2)

@@ -27,15 +27,14 @@ UNITS = [2, 2] + [4] * 14 + [2, 2]
 N_UNITS = len(UNITS)
 FIRST = [sum(UNITS[:c]) for c in range(N_UNITS + 1)]
 LOADS = [4, 4, 4, 4] + [8] * 6
+SCALAR_COLS = 1664
 XT_BANKS = 2
 ACC_BANKS = 2
 OUT_LAG = 4
-GPSIMD_TENTHS = 8
-SCALAR_EIGHTHS = 3
-SCALAR_HEAD = 10
-VECTOR_HEAD = [0, 4, 4, 4]
-STREAM_START = SCALAR_HEAD + sum(VECTOR_HEAD)
-STREAM_QUARTERS = 12
+GPSIMD_TENTHS = 7
+LATE_UNITS = 4
+SCALAR_HEAD = 11
+VECTOR_HEAD = [0, 4, 4]
 assert FIRST[-1] == TILES and sum(LOADS) == TILES
 
 
@@ -193,21 +192,21 @@ def tile_dpn_t_w4_kernel(tc, x_bytes, x_scale, W1_words, W1_scales, b1, W2_words
             n = rows_of(c)
             beside = PACK * rows_of(c + 2) + rows_of(c + 2 - OUT_LAG)
             cut0 = min(n, beside * GPSIMD_TENTHS // 10 // PACK // 16 * 16) if live(c + 2) else 0
-            cut1 = cut0 + ((n - cut0) * SCALAR_EIGHTHS // 8 // 16 * 16 if not live(c + 3) else 0)
+            late = c - (N_UNITS - LATE_UNITS)
+            cut1 = cut0 + ((n - cut0) // 2 if late >= 0 else 0)
             if c not in hg:
-                hg[c] = work.tile([P, MAX_TILES * P, PACK], BF16, name="hg", bufs=1, align_bytes=64)
+                tag = "hg_late%d" % late if late >= 0 else "hg"
+                hg[c] = work.tile([P, MAX_TILES * P, PACK], BF16, name=tag, bufs=1, align_bytes=64)
             rows = {"gpsimd": slice(0, cut0), "scalar": slice(cut0, cut1), "vector": slice(cut1, n)}[engine]
             if rows.start == rows.stop:
                 return
-            run = 2 if engine == "gpsimd" else PACK
-            src = hs[c][:, :, rows].rearrange("p t (n i) -> p n t i", i=run)
-            dst = hg[c][:, rows, :].rearrange("p (n i) t -> p n t i", i=run)
+            src = hs[c][:, :, rows].rearrange("p t n -> p n t")
             if engine == "vector":
-                nc.vector.tensor_copy(out=dst, in_=src)
+                nc.vector.tensor_copy(out=hg[c][:, rows, :], in_=src)
             elif engine == "scalar":
-                nc.scalar.copy(out=dst, in_=src)
+                nc.scalar.copy(out=hg[c][:, rows, :], in_=src)
             else:
-                nc.gpsimd.tensor_scalar(out=dst, in0=src, scalar1=1.0, scalar2=0.0, op0=MULT, op1=ADD)
+                nc.gpsimd.tensor_scalar(out=hg[c][:, rows, :], in0=src, scalar1=1.0, scalar2=0.0, op0=MULT, op1=ADD)
 
         def quantize_h(c):
             if not live(c):
@@ -252,9 +251,6 @@ def tile_dpn_t_w4_kernel(tc, x_bytes, x_scale, W1_words, W1_scales, b1, W2_words
                 in_=ob[c][:, :tiles, :].rearrange("p j o -> p (j o)"),
             )
 
-        def stream_col(s):
-            return D_IN * STREAM_START + D_IN * STREAM_QUARTERS * max(0, s - 1) // 4
-
         widen(0, 2 * D_IN, nc.vector.tensor_copy)
         widen(2 * D_IN, 4 * D_IN, copy_by_activation)
         widen(4 * D_IN, 8 * D_IN, nc.scalar.copy)
@@ -262,18 +258,21 @@ def tile_dpn_t_w4_kernel(tc, x_bytes, x_scale, W1_words, W1_scales, b1, W2_words
         for g in range(XT_BANKS):
             transpose_x(g)
         permute_weights()
+        done = SCALAR_HEAD * D_IN
         for s in range(N_UNITS + OUT_LAG):
-            interleave_h(s - 2, "scalar")
             for t in range(PACK):
                 layer1(s - 1, t)
                 relu(s - 1, t)
-            widen(stream_col(s), stream_col(s + 1), nc.scalar.copy)
+            mid = done + (SCALAR_COLS if s > 0 else 0)
+            widen(done, mid, nc.scalar.copy)
+            interleave_h(s - 1, "scalar")
             interleave_h(s - 2, "gpsimd")
             scale_x(s, 0)
             layer2(s - 3)
             scale_x(s, 2)
             add_b2_and_store(s - OUT_LAG)
             interleave_h(s - 2, "vector")
-            widen((SCALAR_HEAD + sum(VECTOR_HEAD[:s])) * D_IN, (SCALAR_HEAD + sum(VECTOR_HEAD[: s + 1])) * D_IN, nc.vector.tensor_copy)
+            done = mid + (VECTOR_HEAD[s] * D_IN if s < len(VECTOR_HEAD) else 0)
+            widen(mid, done, nc.vector.tensor_copy)
             quantize_x(s)
             quantize_h(s - 2)

@@ -27,14 +27,12 @@ UNITS = [2, 2] + [4] * 14 + [2, 2]
 N_UNITS = len(UNITS)
 FIRST = [sum(UNITS[:c]) for c in range(N_UNITS + 1)]
 LOADS = [4, 4, 4, 4] + [8] * 6
-SCALAR_COLS = 1664
 XT_BANKS = 2
 ACC_BANKS = 2
 OUT_LAG = 4
-GPSIMD_TENTHS = 7
+GPSIMD_SHARE = 13
 LATE_UNITS = 4
-SCALAR_HEAD = 11
-VECTOR_HEAD = [0, 4, 4]
+SCALAR_HEAD = 12
 assert FIRST[-1] == TILES and sum(LOADS) == TILES
 
 
@@ -191,22 +189,24 @@ def tile_dpn_t_w4_kernel(tc, x_bytes, x_scale, W1_words, W1_scales, b1, W2_words
                 return
             n = rows_of(c)
             beside = PACK * rows_of(c + 2) + rows_of(c + 2 - OUT_LAG)
-            cut0 = min(n, beside * GPSIMD_TENTHS // 10 // PACK // 16 * 16) if live(c + 2) else 0
+            cut0 = min(n, beside * GPSIMD_SHARE // 20 // PACK // 16 * 16) if live(c + 2) else 0
             late = c - (N_UNITS - LATE_UNITS)
-            cut1 = cut0 + ((n - cut0) // 2 if late >= 0 else 0)
+            cut1 = cut0 + (n - cut0) // 2 if late >= 0 else n
             if c not in hg:
                 tag = "hg_late%d" % late if late >= 0 else "hg"
                 hg[c] = work.tile([P, MAX_TILES * P, PACK], BF16, name=tag, bufs=1, align_bytes=64)
             rows = {"gpsimd": slice(0, cut0), "scalar": slice(cut0, cut1), "vector": slice(cut1, n)}[engine]
             if rows.start == rows.stop:
                 return
-            src = hs[c][:, :, rows].rearrange("p t n -> p n t")
+            run = 2 if engine == "gpsimd" else 1
+            src = hs[c][:, :, rows].rearrange("p t (n i) -> p n t i", i=run)
+            dst = hg[c][:, rows, :].rearrange("p (n i) t -> p n t i", i=run)
             if engine == "vector":
-                nc.vector.tensor_copy(out=hg[c][:, rows, :], in_=src)
+                nc.vector.tensor_copy(out=dst, in_=src)
             elif engine == "scalar":
-                nc.scalar.copy(out=hg[c][:, rows, :], in_=src)
+                nc.scalar.copy(out=dst, in_=src)
             else:
-                nc.gpsimd.tensor_scalar(out=hg[c][:, rows, :], in0=src, scalar1=1.0, scalar2=0.0, op0=MULT, op1=ADD)
+                nc.gpsimd.tensor_scalar(out=dst, in0=src, scalar1=1.0, scalar2=0.0, op0=MULT, op1=ADD)
 
         def quantize_h(c):
             if not live(c):
@@ -258,21 +258,21 @@ def tile_dpn_t_w4_kernel(tc, x_bytes, x_scale, W1_words, W1_scales, b1, W2_words
         for g in range(XT_BANKS):
             transpose_x(g)
         permute_weights()
-        done = SCALAR_HEAD * D_IN
         for s in range(N_UNITS + OUT_LAG):
+            if s - 2 < N_UNITS - LATE_UNITS:
+                interleave_h(s - 2, "scalar")
             for t in range(PACK):
                 layer1(s - 1, t)
                 relu(s - 1, t)
-            mid = done + (SCALAR_COLS if s > 0 else 0)
-            widen(done, mid, nc.scalar.copy)
-            interleave_h(s - 1, "scalar")
+            if s > 0:
+                widen((SCALAR_HEAD + MAX_TILES * (s - 1)) * D_IN, (SCALAR_HEAD + MAX_TILES * s) * D_IN, nc.scalar.copy)
+            if s - 1 >= N_UNITS - LATE_UNITS:
+                interleave_h(s - 1, "scalar")
             interleave_h(s - 2, "gpsimd")
             scale_x(s, 0)
             layer2(s - 3)
             scale_x(s, 2)
             add_b2_and_store(s - OUT_LAG)
             interleave_h(s - 2, "vector")
-            done = mid + (VECTOR_HEAD[s] * D_IN if s < len(VECTOR_HEAD) else 0)
-            widen(mid, done, nc.vector.tensor_copy)
             quantize_x(s)
             quantize_h(s - 2)

@@ -26,11 +26,11 @@ MAX_TILES = 4
 UNITS = [2, 2] + [4] * 14 + [2, 2]
 N_UNITS = len(UNITS)
 FIRST = [sum(UNITS[:c]) for c in range(N_UNITS + 1)]
-LOADS = [4, 4, 4, 4] + [8] * 6
+LOADS = [2, 4, 4, 6] + [8] * 6
 XT_BANKS = 2
 ACC_BANKS = 2
 OUT_LAG = 4
-GPSIMD_SHARE = 13
+GPSIMD_SHARE = 15
 LATE_UNITS = 4
 SCALAR_HEAD = 12
 assert FIRST[-1] == TILES and sum(LOADS) == TILES
@@ -100,9 +100,11 @@ def tile_dpn_t_w4_kernel(tc, x_bytes, x_scale, W1_words, W1_scales, b1, W2_words
                 in_=w1s_raw[:].rearrange("p (m t) -> p t m", t=PACK),
             )
 
-        xt, xg, xq, xs = {}, {}, {}, {}
+        unit_cols = MAX_TILES * D_IN
+        staged = keep.tile([P, 3 * unit_cols], BF16, name="staged", align_bytes=64)
+        xt, xq, xs = {}, {}, {}
         h, hs, hg, hq, hsc = {}, {}, {}, {}, {}
-        acc, ob = {}, {}
+        acc, ob, bank_of = {}, {}, {}
 
         def live(c):
             return 0 <= c < N_UNITS
@@ -120,12 +122,14 @@ def tile_dpn_t_w4_kernel(tc, x_bytes, x_scale, W1_words, W1_scales, b1, W2_words
         def copy_by_activation(out, in_):
             nc.scalar.activation(out=out, in_=in_, func=COPY)
 
-        def transpose_x(g):
+        def transpose_x(bank):
+            g = len(xt)
             if g >= len(groups):
                 return
             c, j0 = groups[g]
+            bank_of[g] = bank
             words = xb[:].bitcast(F32)
-            xt[g] = psum.tile([P, 2, 2, P], F32, name="xt", bufs=XT_BANKS)
+            xt[g] = psum.tile([P, 2, 2, P], F32, name="xt%d" % bank)
             for j in range(min(2, UNITS[c] - j0)):
                 w0 = (FIRST[c] + j0 + j) * (D_IN // 2)
                 for u in range(2):
@@ -135,12 +139,10 @@ def tile_dpn_t_w4_kernel(tc, x_bytes, x_scale, W1_words, W1_scales, b1, W2_words
             if (c, j0) not in groups:
                 return
             g = groups.index((c, j0))
-            if j0 == 0:
-                xg[c] = work.tile([P, MAX_TILES * D_IN], BF16, name="xg", bufs=2, align_bytes=64)
             n = P * min(2, UNITS[c] - j0)
-            c0 = D_IN * j0
+            c0 = 2 * unit_cols * (c % 2) + D_IN * j0
             nc.vector.tensor_tensor(
-                out=xg[c][:, c0 : c0 + PACK * n].rearrange("p (n u e) -> p n u e", u=2, e=2),
+                out=staged[:, c0 : c0 + PACK * n].rearrange("p (n u e) -> p n u e", u=2, e=2),
                 in0=xt[g][:]
                 .rearrange("p u j n -> p (u j n)")
                 .bitcast(BF16)
@@ -148,17 +150,27 @@ def tile_dpn_t_w4_kernel(tc, x_bytes, x_scale, W1_words, W1_scales, b1, W2_words
                 in1=x_scales[:].rearrange("p (u e) -> p u e", e=2).unsqueeze(1).to_broadcast([P, n, 2, 2]),
                 op=MULT,
             )
-            transpose_x(g + XT_BANKS)
+            transpose_x(bank_of[g])
+
+        def quantize(src, words):
+            codes = work.tile([P, 2 * MAX_TILES * P], U32, name="codes", bufs=9, align_bytes=64)
+            scales = work.tile([P, 2 * MAX_TILES * P], U8, name="scales", bufs=9, align_bytes=64)
+            nc.vector.quantize_mx(out=codes[:, :words].bitcast(FP8X4), scales=scales[:, :words], in_=src)
+            return codes, scales
 
         def quantize_x(c):
             if not live(c):
                 return
-            n = rows_of(c)
-            xq[c] = work.tile([P, MAX_TILES * P], U32, name="xq", bufs=6, align_bytes=64)
-            xs[c] = work.tile([P, MAX_TILES * P], U8, name="xs", bufs=6, align_bytes=64)
-            nc.vector.quantize_mx(
-                out=xq[c][:, :n].bitcast(FP8X4), scales=xs[c][:, :n], in_=xg[c][:, : PACK * n]
-            )
+            c0 = 2 * unit_cols * (c % 2)
+            xq[c], xs[c] = quantize(staged[:, c0 : c0 + PACK * rows_of(c)], rows_of(c))
+
+        def quantize_both(c):
+            n = MAX_TILES * P
+            c0 = unit_cols * (c % 2)
+            codes, scales = quantize(staged[:, c0 : c0 + 2 * unit_cols], 2 * n)
+            x_part, h_part = slice(n * (c % 2), n * (c % 2 + 1)), slice(n * (1 - c % 2), n * (2 - c % 2))
+            xq[c], xs[c] = codes[:, x_part], scales[:, x_part]
+            hq[c - 2], hsc[c - 2] = codes[:, h_part], scales[:, h_part]
 
         def layer1(c, t):
             if not live(c):
@@ -193,14 +205,16 @@ def tile_dpn_t_w4_kernel(tc, x_bytes, x_scale, W1_words, W1_scales, b1, W2_words
             late = c - (N_UNITS - LATE_UNITS)
             cut1 = cut0 + (n - cut0) // 2 if late >= 0 else n
             if c not in hg:
-                tag = "hg_late%d" % late if late >= 0 else "hg"
-                hg[c] = work.tile([P, MAX_TILES * P, PACK], BF16, name=tag, bufs=1, align_bytes=64)
+                if late >= 0:
+                    hg[c] = work.tile([P, unit_cols], BF16, name="hg_late%d" % late, bufs=1, align_bytes=64)
+                else:
+                    hg[c] = staged[:, unit_cols : 2 * unit_cols]
             rows = {"gpsimd": slice(0, cut0), "scalar": slice(cut0, cut1), "vector": slice(cut1, n)}[engine]
             if rows.start == rows.stop:
                 return
             run = 2 if engine == "gpsimd" else 1
             src = hs[c][:, :, rows].rearrange("p t (n i) -> p n t i", i=run)
-            dst = hg[c][:, rows, :].rearrange("p (n i) t -> p n t i", i=run)
+            dst = hg[c][:, PACK * rows.start : PACK * rows.stop].rearrange("p (n i t) -> p n t i", i=run, t=PACK)
             if engine == "vector":
                 nc.vector.tensor_copy(out=dst, in_=src)
             elif engine == "scalar":
@@ -211,12 +225,7 @@ def tile_dpn_t_w4_kernel(tc, x_bytes, x_scale, W1_words, W1_scales, b1, W2_words
         def quantize_h(c):
             if not live(c):
                 return
-            n = rows_of(c)
-            hq[c] = work.tile([P, MAX_TILES * P], U32, name="hq", align_bytes=64)
-            hsc[c] = work.tile([P, MAX_TILES * P], U8, name="hsc", align_bytes=64)
-            nc.vector.quantize_mx(
-                out=hq[c][:, :n].bitcast(FP8X4), scales=hsc[c][:, :n], in_=hg[c][:, :n, :].rearrange("p n t -> p (n t)")
-            )
+            hq[c], hsc[c] = quantize(hg[c][:, : PACK * rows_of(c)], rows_of(c))
 
         def layer2(c):
             if not live(c):
@@ -239,7 +248,7 @@ def tile_dpn_t_w4_kernel(tc, x_bytes, x_scale, W1_words, W1_scales, b1, W2_words
             if not live(c):
                 return
             tiles = UNITS[c]
-            ob[c] = work.tile([P, MAX_TILES, OUT], F32, name="ob")
+            ob[c] = work.tile([P, MAX_TILES, OUT], F32, name="ob", bufs=N_UNITS)
             nc.vector.tensor_tensor(
                 out=ob[c][:, :tiles, :],
                 in0=acc[c][:, :tiles, :],
@@ -251,19 +260,24 @@ def tile_dpn_t_w4_kernel(tc, x_bytes, x_scale, W1_words, W1_scales, b1, W2_words
                 in_=ob[c][:, :tiles, :].rearrange("p j o -> p (j o)"),
             )
 
-        widen(0, 2 * D_IN, nc.vector.tensor_copy)
-        widen(2 * D_IN, 4 * D_IN, copy_by_activation)
-        widen(4 * D_IN, 8 * D_IN, nc.scalar.copy)
-        widen(8 * D_IN, SCALAR_HEAD * D_IN, nc.scalar.copy)
+        widen(0, D_IN, nc.vector.tensor_copy)
+        widen(D_IN, 2 * D_IN, copy_by_activation)
+        widen(2 * D_IN, 4 * D_IN, nc.scalar.copy)
+        widen(4 * D_IN, 6 * D_IN, nc.scalar.copy)
+        widen(6 * D_IN, 10 * D_IN, nc.scalar.copy)
+        widen(10 * D_IN, SCALAR_HEAD * D_IN, nc.scalar.copy)
         for g in range(XT_BANKS):
             transpose_x(g)
         permute_weights()
-        for s in range(N_UNITS + OUT_LAG):
+        def hidden(c):
+            for t in range(PACK):
+                layer1(c, t)
+                relu(c, t)
+
+        def scale_step(s):
             if s - 2 < N_UNITS - LATE_UNITS:
                 interleave_h(s - 2, "scalar")
-            for t in range(PACK):
-                layer1(s - 1, t)
-                relu(s - 1, t)
+            hidden(s - 1)
             if s > 0:
                 widen((SCALAR_HEAD + MAX_TILES * (s - 1)) * D_IN, (SCALAR_HEAD + MAX_TILES * s) * D_IN, nc.scalar.copy)
             if s - 1 >= N_UNITS - LATE_UNITS:
@@ -273,6 +287,33 @@ def tile_dpn_t_w4_kernel(tc, x_bytes, x_scale, W1_words, W1_scales, b1, W2_words
             layer2(s - 3)
             scale_x(s, 2)
             add_b2_and_store(s - OUT_LAG)
+
+        last = N_UNITS - 1
+        for s in range(last):
+            scale_step(s)
             interleave_h(s - 2, "vector")
-            quantize_x(s)
-            quantize_h(s - 2)
+            if s < OUT_LAG:
+                quantize_h(s - 2)
+                quantize_x(s)
+            elif s - 1 < N_UNITS - LATE_UNITS:
+                quantize_both(s)
+            else:
+                quantize_x(s)
+                quantize_h(s - 2)
+        scale_step(last)
+        quantize_x(last)
+        hidden(last)
+        interleave_h(last, "scalar")
+        interleave_h(last - 2, "vector")
+        add_b2_and_store(last - 3)
+        interleave_h(last - 1, "vector")
+        quantize_h(last - 2)
+        layer2(last - 2)
+        quantize_h(last - 1)
+        layer2(last - 1)
+        interleave_h(last, "vector")
+        add_b2_and_store(last - 2)
+        quantize_h(last)
+        layer2(last)
+        add_b2_and_store(last - 1)
+        add_b2_and_store(last)

@@ -27,10 +27,8 @@ UNITS = [2, 2] + [4] * 14 + [2, 2]
 N_UNITS = len(UNITS)
 FIRST = [sum(UNITS[:c]) for c in range(N_UNITS + 1)]
 LOADS = [2, 4, 4, 6] + [8] * 6
-XT_BANKS = 2
-ACC_BANKS = 2
 OUT_LAG = 4
-GPSIMD_SHARE = 15
+GPSIMD_SHARE = 14
 LATE_UNITS = 4
 SCALAR_HEAD = 12
 assert FIRST[-1] == TILES and sum(LOADS) == TILES
@@ -69,11 +67,11 @@ def tile_dpn_t_w4_kernel(tc, x_bytes, x_scale, W1_words, W1_scales, b1, W2_words
         nc.vector.memset(w2s[:].rearrange("p g n -> p (g n)").bitcast(U32), 0)
         load(0)
         nc.scalar.dma_start(out=x_scales[:], in_=x_scale.rearrange("o (p t) -> p (o t)", t=PACK))
-        nc.sync.dma_start(out=w1_raw[:], in_=W1_words[0])
         for q in range(4):
             nc.sync.dma_start(
                 out=w1s_raw[32 * q : 32 * q + 4, :].bitcast(I32), in_=W1_scales[0, 4 * q : 4 * q + 4, :].bitcast(I32)
             )
+        nc.sync.dma_start(out=w1_raw[:], in_=W1_words[0])
         make_identity(nc, ident[:])
         load(1)
         load(2)
@@ -90,11 +88,13 @@ def tile_dpn_t_w4_kernel(tc, x_bytes, x_scale, W1_words, W1_scales, b1, W2_words
         for i in range(5, len(LOADS)):
             load(i)
 
-        def permute_weights():
+        def permute_codes():
             nc.vector.tensor_copy(
                 out=w1[:].rearrange("p (t m b) -> p t m b", t=PACK, b=2),
                 in_=w1_raw[:].rearrange("p (m t b) -> p t m b", t=PACK, b=2),
             )
+
+        def permute_scales():
             nc.vector.tensor_copy(
                 out=w1s[:].rearrange("p (t m) -> p t m", t=PACK),
                 in_=w1s_raw[:].rearrange("p (m t) -> p t m", t=PACK),
@@ -112,7 +112,7 @@ def tile_dpn_t_w4_kernel(tc, x_bytes, x_scale, W1_words, W1_scales, b1, W2_words
         def rows_of(c):
             return P * UNITS[c] if live(c) else 0
 
-        groups = [(c, j) for c in range(N_UNITS) for j in range(0, UNITS[c], 2)]
+        groups = [(0, 0, 1), (0, 1, 1)] + [(c, j, min(2, UNITS[c] - j)) for c in range(1, N_UNITS) for j in range(0, UNITS[c], 2)]
 
         def widen(lo, hi, copy):
             cols = slice(lo, min(hi, TILES * D_IN))
@@ -126,20 +126,21 @@ def tile_dpn_t_w4_kernel(tc, x_bytes, x_scale, W1_words, W1_scales, b1, W2_words
             g = len(xt)
             if g >= len(groups):
                 return
-            c, j0 = groups[g]
+            c, j0, tiles = groups[g]
             bank_of[g] = bank
             words = xb[:].bitcast(F32)
-            xt[g] = psum.tile([P, 2, 2, P], F32, name="xt%d" % bank)
-            for j in range(min(2, UNITS[c] - j0)):
+            xt[g] = psum.tile([P, 2, 2, P], F32, name=bank)
+            for j in range(tiles):
                 w0 = (FIRST[c] + j0 + j) * (D_IN // 2)
                 for u in range(2):
                     nc.tensor.transpose(xt[g][:, u, j, :], words[:, w0 + u : w0 + D_IN // 2 : 2], ident[:])
 
-        def scale_x(c, j0):
-            if (c, j0) not in groups:
+        def scale_x(c, j0, refill=True):
+            starts = [group[:2] for group in groups]
+            if (c, j0) not in starts:
                 return
-            g = groups.index((c, j0))
-            n = P * min(2, UNITS[c] - j0)
+            g = starts.index((c, j0))
+            n = P * groups[g][2]
             c0 = 2 * unit_cols * (c % 2) + D_IN * j0
             nc.vector.tensor_tensor(
                 out=staged[:, c0 : c0 + PACK * n].rearrange("p (n u e) -> p n u e", u=2, e=2),
@@ -150,7 +151,8 @@ def tile_dpn_t_w4_kernel(tc, x_bytes, x_scale, W1_words, W1_scales, b1, W2_words
                 in1=x_scales[:].rearrange("p (u e) -> p u e", e=2).unsqueeze(1).to_broadcast([P, n, 2, 2]),
                 op=MULT,
             )
-            transpose_x(bank_of[g])
+            if refill:
+                transpose_x(bank_of[g])
 
         def quantize(src, words):
             codes = work.tile([P, 2 * MAX_TILES * P], U32, name="codes", bufs=9, align_bytes=64)
@@ -227,10 +229,10 @@ def tile_dpn_t_w4_kernel(tc, x_bytes, x_scale, W1_words, W1_scales, b1, W2_words
                 return
             hq[c], hsc[c] = quantize(hg[c][:, : PACK * rows_of(c)], rows_of(c))
 
-        def layer2(c):
+        def layer2(c, bank=None):
             if not live(c):
                 return
-            acc[c] = psum.tile([P, MAX_TILES, OUT], F32, name="acc", bufs=ACC_BANKS)
+            acc[c] = psum.tile([P, MAX_TILES, OUT], F32, name=bank or "acc%d" % (c % 2))
             for j in range(UNITS[c]):
                 cols = slice(P * j, P * (j + 1))
                 for g, codes, scales in ((0, xq[c], xs[c]), (1, hq[c], hsc[c])):
@@ -266,9 +268,6 @@ def tile_dpn_t_w4_kernel(tc, x_bytes, x_scale, W1_words, W1_scales, b1, W2_words
         widen(4 * D_IN, 6 * D_IN, nc.scalar.copy)
         widen(6 * D_IN, 10 * D_IN, nc.scalar.copy)
         widen(10 * D_IN, SCALAR_HEAD * D_IN, nc.scalar.copy)
-        for g in range(XT_BANKS):
-            transpose_x(g)
-        permute_weights()
         def hidden(c):
             for t in range(PACK):
                 layer1(c, t)
@@ -278,8 +277,7 @@ def tile_dpn_t_w4_kernel(tc, x_bytes, x_scale, W1_words, W1_scales, b1, W2_words
             if s - 2 < N_UNITS - LATE_UNITS:
                 interleave_h(s - 2, "scalar")
             hidden(s - 1)
-            if s > 0:
-                widen((SCALAR_HEAD + MAX_TILES * (s - 1)) * D_IN, (SCALAR_HEAD + MAX_TILES * s) * D_IN, nc.scalar.copy)
+            widen((SCALAR_HEAD + MAX_TILES * (s - 1)) * D_IN, (SCALAR_HEAD + MAX_TILES * s) * D_IN, nc.scalar.copy)
             if s - 1 >= N_UNITS - LATE_UNITS:
                 interleave_h(s - 1, "scalar")
             interleave_h(s - 2, "gpsimd")
@@ -289,7 +287,28 @@ def tile_dpn_t_w4_kernel(tc, x_bytes, x_scale, W1_words, W1_scales, b1, W2_words
             add_b2_and_store(s - OUT_LAG)
 
         last = N_UNITS - 1
-        for s in range(last):
+        for bank in ("xt0", "xt1", "acc0", "acc1"):
+            transpose_x(bank)
+        permute_codes()
+        scale_x(0, 0, refill=False)
+        scale_x(0, 1, refill=False)
+        permute_scales()
+        quantize_x(0)
+        hidden(0)
+        transpose_x("xt0")
+        widen(SCALAR_HEAD * D_IN, (SCALAR_HEAD + MAX_TILES) * D_IN, nc.scalar.copy)
+        scale_x(1, 0, refill=False)
+        scale_x(2, 0, refill=False)
+        quantize_x(1)
+        transpose_x("xt1")
+        hidden(1)
+        widen((SCALAR_HEAD + MAX_TILES) * D_IN, (SCALAR_HEAD + 2 * MAX_TILES) * D_IN, nc.scalar.copy)
+        interleave_h(0, "scalar")
+        interleave_h(0, "gpsimd")
+        scale_x(2, 2)
+        quantize_h(0)
+        quantize_x(2)
+        for s in range(3, last):
             scale_step(s)
             interleave_h(s - 2, "vector")
             if s < OUT_LAG:
@@ -312,8 +331,8 @@ def tile_dpn_t_w4_kernel(tc, x_bytes, x_scale, W1_words, W1_scales, b1, W2_words
         quantize_h(last - 1)
         layer2(last - 1)
         interleave_h(last, "vector")
-        add_b2_and_store(last - 2)
-        quantize_h(last)
-        layer2(last)
         add_b2_and_store(last - 1)
+        quantize_h(last)
+        layer2(last, "xt0")
+        add_b2_and_store(last - 2)
         add_b2_and_store(last)

@@ -31,6 +31,8 @@ OUT_LAG = 4
 GPSIMD_SHARE = 14
 LATE_UNITS = 4
 SCALAR_HEAD = 12
+HEAD_COLS = 1024
+STREAM_COLS = 2048
 assert FIRST[-1] == TILES and sum(LOADS) == TILES
 
 
@@ -66,7 +68,7 @@ def tile_dpn_t_w4_kernel(tc, x_bytes, x_scale, W1_words, W1_scales, b1, W2_words
         nc.vector.memset(w1s_raw[:].bitcast(U32), 0)
         nc.vector.memset(w2s[:].rearrange("p g n -> p (g n)").bitcast(U32), 0)
         load(0)
-        nc.scalar.dma_start(out=x_scales[:], in_=x_scale.rearrange("o (p t) -> p (o t)", t=PACK))
+        nc.sync.dma_start(out=x_scales[:], in_=x_scale.rearrange("o (p t) -> p (o t)", t=PACK))
         for q in range(4):
             nc.sync.dma_start(
                 out=w1s_raw[32 * q : 32 * q + 4, :].bitcast(I32), in_=W1_scales[0, 4 * q : 4 * q + 4, :].bitcast(I32)
@@ -214,7 +216,7 @@ def tile_dpn_t_w4_kernel(tc, x_bytes, x_scale, W1_words, W1_scales, b1, W2_words
             rows = {"gpsimd": slice(0, cut0), "scalar": slice(cut0, cut1), "vector": slice(cut1, n)}[engine]
             if rows.start == rows.stop:
                 return
-            run = 2 if engine == "gpsimd" else 1
+            run = 2 if engine == "gpsimd" else 4
             src = hs[c][:, :, rows].rearrange("p t (n i) -> p n t i", i=run)
             dst = hg[c][:, PACK * rows.start : PACK * rows.stop].rearrange("p (n i t) -> p n t i", i=run, t=PACK)
             if engine == "vector":
@@ -268,6 +270,9 @@ def tile_dpn_t_w4_kernel(tc, x_bytes, x_scale, W1_words, W1_scales, b1, W2_words
         widen(4 * D_IN, 6 * D_IN, nc.scalar.copy)
         widen(6 * D_IN, 10 * D_IN, nc.scalar.copy)
         widen(10 * D_IN, SCALAR_HEAD * D_IN, nc.scalar.copy)
+        def stream_col(s):
+            return SCALAR_HEAD * D_IN + HEAD_COLS * min(s, 2) + STREAM_COLS * max(s - 2, 0)
+
         def hidden(c):
             for t in range(PACK):
                 layer1(c, t)
@@ -277,7 +282,7 @@ def tile_dpn_t_w4_kernel(tc, x_bytes, x_scale, W1_words, W1_scales, b1, W2_words
             if s - 2 < N_UNITS - LATE_UNITS:
                 interleave_h(s - 2, "scalar")
             hidden(s - 1)
-            widen((SCALAR_HEAD + MAX_TILES * (s - 1)) * D_IN, (SCALAR_HEAD + MAX_TILES * s) * D_IN, nc.scalar.copy)
+            widen(stream_col(s - 1), stream_col(s), nc.scalar.copy)
             if s - 1 >= N_UNITS - LATE_UNITS:
                 interleave_h(s - 1, "scalar")
             interleave_h(s - 2, "gpsimd")
@@ -296,18 +301,18 @@ def tile_dpn_t_w4_kernel(tc, x_bytes, x_scale, W1_words, W1_scales, b1, W2_words
         quantize_x(0)
         hidden(0)
         transpose_x("xt0")
-        widen(SCALAR_HEAD * D_IN, (SCALAR_HEAD + MAX_TILES) * D_IN, nc.scalar.copy)
+        widen(stream_col(0), stream_col(1), nc.scalar.copy)
         scale_x(1, 0, refill=False)
         scale_x(2, 0, refill=False)
         quantize_x(1)
         transpose_x("xt1")
         hidden(1)
-        widen((SCALAR_HEAD + MAX_TILES) * D_IN, (SCALAR_HEAD + 2 * MAX_TILES) * D_IN, nc.scalar.copy)
+        widen(stream_col(1), stream_col(2), nc.scalar.copy)
         interleave_h(0, "scalar")
         interleave_h(0, "gpsimd")
         scale_x(2, 2)
-        quantize_h(0)
         quantize_x(2)
+        quantize_h(0)
         for s in range(3, last):
             scale_step(s)
             interleave_h(s - 2, "vector")

@@ -28,7 +28,7 @@ N_UNITS = len(UNITS)
 FIRST = [sum(UNITS[:c]) for c in range(N_UNITS + 1)]
 LOADS = [2, 4, 4, 6] + [8] * 6
 OUT_LAG = 4
-GPSIMD_SHARE = 14
+GPSIMD_SHARE = 15
 LATE_UNITS = 4
 SCALAR_HEAD = 12
 HEAD_COLS = 1024
@@ -143,7 +143,7 @@ def tile_dpn_t_w4_kernel(tc, x_bytes, x_scale, W1_words, W1_scales, b1, W2_words
                 return
             g = starts.index((c, j0))
             n = P * groups[g][2]
-            c0 = 2 * unit_cols * (c % 2) + D_IN * j0
+            c0 = unit_cols * (c % 3) + D_IN * j0
             nc.vector.tensor_tensor(
                 out=staged[:, c0 : c0 + PACK * n].rearrange("p (n u e) -> p n u e", u=2, e=2),
                 in0=xt[g][:]
@@ -157,24 +157,16 @@ def tile_dpn_t_w4_kernel(tc, x_bytes, x_scale, W1_words, W1_scales, b1, W2_words
                 transpose_x(bank_of[g])
 
         def quantize(src, words):
-            codes = work.tile([P, 2 * MAX_TILES * P], U32, name="codes", bufs=9, align_bytes=64)
-            scales = work.tile([P, 2 * MAX_TILES * P], U8, name="scales", bufs=9, align_bytes=64)
+            codes = work.tile([P, MAX_TILES * P], U32, name="codes", bufs=12, align_bytes=64)
+            scales = work.tile([P, MAX_TILES * P], U8, name="scales", bufs=12, align_bytes=64)
             nc.vector.quantize_mx(out=codes[:, :words].bitcast(FP8X4), scales=scales[:, :words], in_=src)
             return codes, scales
 
         def quantize_x(c):
             if not live(c):
                 return
-            c0 = 2 * unit_cols * (c % 2)
+            c0 = unit_cols * (c % 3)
             xq[c], xs[c] = quantize(staged[:, c0 : c0 + PACK * rows_of(c)], rows_of(c))
-
-        def quantize_both(c):
-            n = MAX_TILES * P
-            c0 = unit_cols * (c % 2)
-            codes, scales = quantize(staged[:, c0 : c0 + 2 * unit_cols], 2 * n)
-            x_part, h_part = slice(n * (c % 2), n * (c % 2 + 1)), slice(n * (1 - c % 2), n * (2 - c % 2))
-            xq[c], xs[c] = codes[:, x_part], scales[:, x_part]
-            hq[c - 2], hsc[c - 2] = codes[:, h_part], scales[:, h_part]
 
         def layer1(c, t):
             if not live(c):
@@ -212,7 +204,8 @@ def tile_dpn_t_w4_kernel(tc, x_bytes, x_scale, W1_words, W1_scales, b1, W2_words
                 if late >= 0:
                     hg[c] = work.tile([P, unit_cols], BF16, name="hg_late%d" % late, bufs=1, align_bytes=64)
                 else:
-                    hg[c] = staged[:, unit_cols : 2 * unit_cols]
+                    r0 = unit_cols * ((c + 1) % 3)
+                    hg[c] = staged[:, r0 : r0 + unit_cols]
             rows = {"gpsimd": slice(0, cut0), "scalar": slice(cut0, cut1), "vector": slice(cut1, n)}[engine]
             if rows.start == rows.stop:
                 return
@@ -319,8 +312,6 @@ def tile_dpn_t_w4_kernel(tc, x_bytes, x_scale, W1_words, W1_scales, b1, W2_words
             if s < OUT_LAG:
                 quantize_h(s - 2)
                 quantize_x(s)
-            elif s - 1 < N_UNITS - LATE_UNITS:
-                quantize_both(s)
             else:
                 quantize_x(s)
                 quantize_h(s - 2)

@@ -16,24 +16,19 @@ FP8X4 = mybir.dt.float8_e4m3fn_x4
 FP4X4 = mybir.dt.float4_e2m1fn_x4
 ADD = mybir.AluOpType.add
 MULT = mybir.AluOpType.mult
+MAX = mybir.AluOpType.max
 RELU = mybir.ActivationFunctionType.Relu
 COPY = mybir.ActivationFunctionType.Copy
 
 P = 128
 PACK = 4
 TILES = ROWS // P
-MAX_TILES = 4
-UNITS = [2, 2] + [4] * 14 + [2, 2]
-N_UNITS = len(UNITS)
-FIRST = [sum(UNITS[:c]) for c in range(N_UNITS + 1)]
-LOADS = [2, 4, 4, 6] + [8] * 6
-OUT_LAG = 4
-GPSIMD_SHARE = 15
-LATE_UNITS = 4
-SCALAR_HEAD = 12
-HEAD_COLS = 1024
-STREAM_COLS = 2048
-assert FIRST[-1] == TILES and sum(LOADS) == TILES
+RING = 12
+SPARE = -2
+H_RING = 16
+LOADS = [2, 4, 6, 6, 6] + [8] * 5
+G_ROWS = 464
+assert sum(LOADS) == TILES
 
 
 def tile_dpn_t_w4_kernel(tc, x_bytes, x_scale, W1_words, W1_scales, b1, W2_words, W2_scales, b2, out):
@@ -57,6 +52,12 @@ def tile_dpn_t_w4_kernel(tc, x_bytes, x_scale, W1_words, W1_scales, b1, W2_words
         b2_row = keep.tile([P, OUT], BF16, name="b2_row")
         x8 = keep.tile([P, TILES * D_IN], U8, name="x8", align_bytes=64)
         xb = keep.tile([P, TILES * D_IN], BF16, name="xb", align_bytes=64)
+        staged = keep.tile([P, (RING + 2) * D_IN], BF16, name="staged", align_bytes=64)
+        x_codes = keep.tile([P, ROWS], U32, name="x_codes", align_bytes=64)
+        x_exps = keep.tile([P, ROWS], U8, name="x_exps", align_bytes=64)
+        h_codes = keep.tile([P, H_RING * P], U32, name="h_codes", align_bytes=64)
+        h_exps = keep.tile([P, H_RING * P], U8, name="h_exps", align_bytes=64)
+        result = keep.tile([P, TILES * OUT], F32, name="result")
 
         x_rows = x_bytes.rearrange("(p j) k -> p (j k)", j=TILES)
         out_rows = out.rearrange("(p j) o -> p (j o)", j=TILES)
@@ -65,27 +66,24 @@ def tile_dpn_t_w4_kernel(tc, x_bytes, x_scale, W1_words, W1_scales, b1, W2_words
             cols = slice(D_IN * sum(LOADS[:i]), D_IN * sum(LOADS[: i + 1]))
             nc.sync.dma_start(out=x8[:, cols], in_=x_rows[:, cols])
 
+        def load_scale_rows(dst, src):
+            for q in range(4):
+                nc.sync.dma_start(out=dst[32 * q : 32 * q + 4].bitcast(I32), in_=src[4 * q : 4 * q + 4])
+
         nc.vector.memset(w1s_raw[:].bitcast(U32), 0)
         nc.vector.memset(w2s[:].rearrange("p g n -> p (g n)").bitcast(U32), 0)
         load(0)
-        nc.sync.dma_start(out=x_scales[:], in_=x_scale.rearrange("o (p t) -> p (o t)", t=PACK))
-        for q in range(4):
-            nc.sync.dma_start(
-                out=w1s_raw[32 * q : 32 * q + 4, :].bitcast(I32), in_=W1_scales[0, 4 * q : 4 * q + 4, :].bitcast(I32)
-            )
         nc.sync.dma_start(out=w1_raw[:], in_=W1_words[0])
-        make_identity(nc, ident[:])
         load(1)
+        nc.sync.dma_start(out=x_scales[:], in_=x_scale.rearrange("o (p t) -> p (o t)", t=PACK))
+        load_scale_rows(w1s_raw, W1_scales[0].bitcast(I32))
+        make_identity(nc, ident[:])
         load(2)
         nc.sync.dma_start(out=b1_col[:], in_=b1.rearrange("(p t) -> p t", t=PACK))
         load(3)
         load(4)
         nc.sync.dma_start(out=w2[:], in_=W2_words.rearrange("g p n -> p g n"))
-        for q in range(4):
-            nc.sync.dma_start(
-                out=w2s[32 * q : 32 * q + 4, :, :].bitcast(I32),
-                in_=W2_scales.bitcast(I32)[:, 4 * q : 4 * q + 4, :].rearrange("g q n -> q g n"),
-            )
+        load_scale_rows(w2s, W2_scales.bitcast(I32).rearrange("g q n -> q g n"))
         nc.sync.dma_start(out=b2_row[:], in_=b2.partition_broadcast(P))
         for i in range(5, len(LOADS)):
             load(i)
@@ -102,233 +100,243 @@ def tile_dpn_t_w4_kernel(tc, x_bytes, x_scale, W1_words, W1_scales, b1, W2_words
                 in_=w1s_raw[:].rearrange("p (m t) -> p t m", t=PACK),
             )
 
-        unit_cols = MAX_TILES * D_IN
-        staged = keep.tile([P, 3 * unit_cols], BF16, name="staged", align_bytes=64)
-        xt, xq, xs = {}, {}, {}
-        h, hs, hg, hq, hsc = {}, {}, {}, {}, {}
-        acc, ob, bank_of = {}, {}, {}
+        turned, hidden, planes, sums = {}, {}, {}, {}
 
-        def live(c):
-            return 0 <= c < N_UNITS
-
-        def rows_of(c):
-            return P * UNITS[c] if live(c) else 0
-
-        groups = [(0, 0, 1), (0, 1, 1)] + [(c, j, min(2, UNITS[c] - j)) for c in range(1, N_UNITS) for j in range(0, UNITS[c], 2)]
-
-        def widen(lo, hi, copy):
-            cols = slice(lo, min(hi, TILES * D_IN))
+        def widen(a, b, copy=nc.scalar.copy):
+            cols = slice(int(D_IN * a), int(D_IN * min(b, TILES)))
             if cols.start < cols.stop:
                 copy(out=xb[:, cols], in_=x8[:, cols].bitcast(FP8))
 
         def copy_by_activation(out, in_):
             nc.scalar.activation(out=out, in_=in_, func=COPY)
 
-        def transpose_x(bank):
-            g = len(xt)
-            if g >= len(groups):
+        def turn(a, b, bank):
+            if a >= TILES:
                 return
-            c, j0, tiles = groups[g]
-            bank_of[g] = bank
             words = xb[:].bitcast(F32)
-            xt[g] = psum.tile([P, 2, 2, P], F32, name=bank)
-            for j in range(tiles):
-                w0 = (FIRST[c] + j0 + j) * (D_IN // 2)
+            turned[a] = psum.tile([P, 2, 2, P], F32, name=bank)
+            for j in range(b - a):
+                w0 = (a + j) * (D_IN // 2)
                 for u in range(2):
-                    nc.tensor.transpose(xt[g][:, u, j, :], words[:, w0 + u : w0 + D_IN // 2 : 2], ident[:])
+                    nc.tensor.transpose(turned[a][:, u, j, :], words[:, w0 + u : w0 + D_IN // 2 : 2], ident[:])
 
-        def scale_x(c, j0, refill=True):
-            starts = [group[:2] for group in groups]
-            if (c, j0) not in starts:
-                return
-            g = starts.index((c, j0))
-            n = P * groups[g][2]
-            c0 = unit_cols * (c % 3) + D_IN * j0
+        def ring(a, b):
+            a0 = RING if a == SPARE else a % RING
+            return staged[:, D_IN * a0 : D_IN * (a0 + b - a)]
+
+        def scale_x(a, b, first=None):
+            first = a if first is None else first
+            n, n0 = P * (b - a), P * (a - first)
             nc.vector.tensor_tensor(
-                out=staged[:, c0 : c0 + PACK * n].rearrange("p (n u e) -> p n u e", u=2, e=2),
-                in0=xt[g][:]
+                out=ring(a, b).rearrange("p (n u e) -> p n u e", u=2, e=2),
+                in0=turned[first][:]
                 .rearrange("p u j n -> p (u j n)")
                 .bitcast(BF16)
-                .rearrange("p (u n e) -> p n u e", u=2, e=2)[:, :n],
+                .rearrange("p (u n e) -> p n u e", u=2, e=2)[:, n0 : n0 + n],
                 in1=x_scales[:].rearrange("p (u e) -> p u e", e=2).unsqueeze(1).to_broadcast([P, n, 2, 2]),
                 op=MULT,
             )
-            if refill:
-                transpose_x(bank_of[g])
 
-        def quantize(src, words):
-            codes = work.tile([P, MAX_TILES * P], U32, name="codes", bufs=12, align_bytes=64)
-            scales = work.tile([P, MAX_TILES * P], U8, name="scales", bufs=12, align_bytes=64)
-            nc.vector.quantize_mx(out=codes[:, :words].bitcast(FP8X4), scales=scales[:, :words], in_=src)
-            return codes, scales
+        def quantize(codes, exps, a, b, src):
+            rows = slice(P * a, P * b)
+            nc.vector.quantize_mx(out=codes[:, rows].bitcast(FP8X4), scales=exps[:, rows], in_=src)
 
-        def quantize_x(c):
-            if not live(c):
-                return
-            c0 = unit_cols * (c % 3)
-            xq[c], xs[c] = quantize(staged[:, c0 : c0 + PACK * rows_of(c)], rows_of(c))
+        def quantize_x(a, b):
+            quantize(x_codes, x_exps, a, b, ring(a, b))
 
-        def layer1(c, t):
-            if not live(c):
-                return
-            n = rows_of(c)
-            h[c, t] = psum.tile([P, MAX_TILES * P], F32, name="h%d" % t)
+        def quantize_h(a, b, slot):
+            quantize(h_codes, h_exps, a % H_RING, a % H_RING + b - a, ring(slot, slot + b - a))
+
+        def layer1(a, b, t, bank):
+            n = P * (b - a)
+            if isinstance(bank, str):
+                tile = psum.tile([P, 4 * P], F32, name=bank)
+                hidden[a, t] = tile, 0
+            else:
+                hidden[a, t] = hidden[a, bank][0], hidden[a, bank][1] + n
+            tile, c0 = hidden[a, t]
             nc.tensor.matmul_mx(
-                out=h[c, t][:, :n],
+                out=tile[:, c0 : c0 + n],
                 lhsT=w1[:, 2 * P * t : 2 * P * (t + 1)].bitcast(FP4X4),
                 lhsT_scale=w1s[:, P * t : P * (t + 1)],
-                rhs=xq[c][:, :n].bitcast(FP8X4),
-                rhs_scale=xs[c][:, :n],
+                rhs=x_codes[:, P * a : P * b].bitcast(FP8X4),
+                rhs_scale=x_exps[:, P * a : P * b],
                 start=True,
                 stop=True,
             )
 
-        def relu(c, t):
-            if not live(c):
-                return
-            n = rows_of(c)
-            if c not in hs:
-                hs[c] = work.tile([P, PACK, MAX_TILES * P], BF16, name="hs", align_bytes=64)
-            dst = hs[c][:, t, :n]
-            nc.scalar.activation(out=dst, in_=h[c, t][:, :n], func=RELU, bias=b1_col[:, t : t + 1])
+        def relu(a, b, t, on_vector=False, into=None, first=None):
+            into = a if into is None else into
+            n, n0 = P * (b - a), 4 * P * t + P * (a - into)
+            if into not in planes:
+                planes[into] = work.tile([P, PACK * 4 * P], BF16, name="planes", bufs=4, align_bytes=64)
+            first = a if first is None else first
+            tile, c0 = hidden[first, t]
+            c0 = c0 + P * (a - first)
+            dst, src = planes[into][:, n0 : n0 + n], tile[:, c0 : c0 + n]
+            if on_vector:
+                nc.vector.tensor_scalar(out=dst, in0=src, scalar1=b1_col[:, t : t + 1], scalar2=0.0, op0=ADD, op1=MAX)
+            else:
+                nc.scalar.activation(out=dst, in_=src, func=RELU, bias=b1_col[:, t : t + 1])
 
-        def interleave_h(c, engine):
-            if not live(c):
+        def interleave(a, b, slot, r0, r1, engine):
+            if r0 >= r1:
                 return
-            n = rows_of(c)
-            beside = PACK * rows_of(c + 2) + rows_of(c + 2 - OUT_LAG)
-            cut0 = min(n, beside * GPSIMD_SHARE // 20 // PACK // 16 * 16) if live(c + 2) else 0
-            late = c - (N_UNITS - LATE_UNITS)
-            cut1 = cut0 + (n - cut0) // 2 if late >= 0 else n
-            if c not in hg:
-                if late >= 0:
-                    hg[c] = work.tile([P, unit_cols], BF16, name="hg_late%d" % late, bufs=1, align_bytes=64)
-                else:
-                    r0 = unit_cols * ((c + 1) % 3)
-                    hg[c] = staged[:, r0 : r0 + unit_cols]
-            rows = {"gpsimd": slice(0, cut0), "scalar": slice(cut0, cut1), "vector": slice(cut1, n)}[engine]
-            if rows.start == rows.stop:
-                return
-            run = 2 if engine == "gpsimd" else 4
-            src = hs[c][:, :, rows].rearrange("p t (n i) -> p n t i", i=run)
-            dst = hg[c][:, PACK * rows.start : PACK * rows.stop].rearrange("p (n i t) -> p n t i", i=run, t=PACK)
-            if engine == "vector":
+            run = 2 if engine is nc.gpsimd else 4
+            src = planes[a][:].rearrange("p (t n) -> p t n", t=PACK)[:, :, r0:r1]
+            src = src.rearrange("p t (n i) -> p n t i", i=run)
+            dst = ring(slot, slot + b - a)[:, PACK * r0 : PACK * r1].rearrange("p (n i t) -> p n t i", i=run, t=PACK)
+            if engine is nc.vector:
                 nc.vector.tensor_copy(out=dst, in_=src)
-            elif engine == "scalar":
+            elif engine is nc.scalar:
                 nc.scalar.copy(out=dst, in_=src)
             else:
                 nc.gpsimd.tensor_scalar(out=dst, in0=src, scalar1=1.0, scalar2=0.0, op0=MULT, op1=ADD)
 
-        def quantize_h(c):
-            if not live(c):
-                return
-            hq[c], hsc[c] = quantize(hg[c][:, : PACK * rows_of(c)], rows_of(c))
-
-        def layer2(c, bank=None):
-            if not live(c):
-                return
-            acc[c] = psum.tile([P, MAX_TILES, OUT], F32, name=bank or "acc%d" % (c % 2))
-            for j in range(UNITS[c]):
-                cols = slice(P * j, P * (j + 1))
-                for g, codes, scales in ((0, xq[c], xs[c]), (1, hq[c], hsc[c])):
+        def layer2(a, b, bank):
+            sums[a] = psum.tile([P, 4, OUT], F32, name=bank)
+            for j in range(a, b):
+                for g, codes, exps, col in ((0, x_codes, x_exps, j), (1, h_codes, h_exps, j % H_RING)):
+                    cols = slice(P * col, P * (col + 1))
                     nc.tensor.matmul_mx(
-                        out=acc[c][:, j, :],
+                        out=sums[a][:, j - a, :],
                         lhsT=codes[:, cols].bitcast(FP8X4),
-                        lhsT_scale=scales[:, cols],
+                        lhsT_scale=exps[:, cols],
                         rhs=w2[:, g, :].bitcast(FP4X4),
                         rhs_scale=w2s[:, g, :],
                         start=(g == 0),
                         stop=(g == 1),
                     )
 
-        def add_b2_and_store(c):
-            if not live(c):
-                return
-            tiles = UNITS[c]
-            ob[c] = work.tile([P, MAX_TILES, OUT], F32, name="ob", bufs=N_UNITS)
+        def add_b2_and_store(a, b, first=None):
+            first = a if first is None else first
+            dst = result[:, OUT * a : OUT * b]
             nc.vector.tensor_tensor(
-                out=ob[c][:, :tiles, :],
-                in0=acc[c][:, :tiles, :],
-                in1=b2_row[:].unsqueeze(1).to_broadcast([P, tiles, OUT]),
+                out=dst.rearrange("p (j o) -> p j o", o=OUT),
+                in0=sums[first][:, a - first : b - first, :],
+                in1=b2_row[:].unsqueeze(1).to_broadcast([P, b - a, OUT]),
                 op=ADD,
             )
-            nc.sync.dma_start(
-                out=out_rows[:, OUT * FIRST[c] : OUT * FIRST[c + 1]],
-                in_=ob[c][:, :tiles, :].rearrange("p j o -> p (j o)"),
-            )
+            nc.sync.dma_start(out=out_rows[:, OUT * a : OUT * b], in_=dst)
 
-        widen(0, D_IN, nc.vector.tensor_copy)
-        widen(D_IN, 2 * D_IN, copy_by_activation)
-        widen(2 * D_IN, 4 * D_IN, nc.scalar.copy)
-        widen(4 * D_IN, 6 * D_IN, nc.scalar.copy)
-        widen(6 * D_IN, 10 * D_IN, nc.scalar.copy)
-        widen(10 * D_IN, SCALAR_HEAD * D_IN, nc.scalar.copy)
-        def stream_col(s):
-            return SCALAR_HEAD * D_IN + HEAD_COLS * min(s, 2) + STREAM_COLS * max(s - 2, 0)
-
-        def hidden(c):
+        def hidden_in_halves(a):
             for t in range(PACK):
-                layer1(c, t)
-                relu(c, t)
+                layer1(a, a + 4, t, "h%d" % t)
+                relu(a, a + 2, t)
+            for t in range(PACK):
+                relu(a + 2, a + 4, t, first=a)
 
-        def scale_step(s):
-            if s - 2 < N_UNITS - LATE_UNITS:
-                interleave_h(s - 2, "scalar")
-            hidden(s - 1)
-            widen(stream_col(s - 1), stream_col(s), nc.scalar.copy)
-            if s - 1 >= N_UNITS - LATE_UNITS:
-                interleave_h(s - 1, "scalar")
-            interleave_h(s - 2, "gpsimd")
-            scale_x(s, 0)
-            layer2(s - 3)
-            scale_x(s, 2)
-            add_b2_and_store(s - OUT_LAG)
+        def hidden_on_scalar(a, b, ts=range(PACK), into=None):
+            for t in ts:
+                layer1(a, b, t, "h%d" % t)
+                relu(a, b, t, into=into)
 
-        last = N_UNITS - 1
-        for bank in ("xt0", "xt1", "acc0", "acc1"):
-            transpose_x(bank)
+        S, V, G = nc.scalar, nc.vector, nc.gpsimd
+
+        widen(0, 1, nc.vector.tensor_copy)
+        widen(1, 2, copy_by_activation)
+        widen(2, 4)
+        widen(4, 6)
+        widen(6, 9)
+        widen(9, 12)
+        turn(0, 1, "xt0")
+        turn(1, 2, "xt1")
+        turn(2, 4, "acc0")
+        turn(4, 6, "acc1")
         permute_codes()
-        scale_x(0, 0, refill=False)
-        scale_x(0, 1, refill=False)
+        scale_x(0, 1)
+        scale_x(1, 2)
         permute_scales()
-        quantize_x(0)
-        hidden(0)
-        transpose_x("xt0")
-        widen(stream_col(0), stream_col(1), nc.scalar.copy)
-        scale_x(1, 0, refill=False)
-        scale_x(2, 0, refill=False)
-        quantize_x(1)
-        transpose_x("xt1")
-        hidden(1)
-        widen(stream_col(1), stream_col(2), nc.scalar.copy)
-        interleave_h(0, "scalar")
-        interleave_h(0, "gpsimd")
-        scale_x(2, 2)
-        quantize_x(2)
-        quantize_h(0)
-        for s in range(3, last):
-            scale_step(s)
-            interleave_h(s - 2, "vector")
-            if s < OUT_LAG:
-                quantize_h(s - 2)
-                quantize_x(s)
+        quantize_x(0, 2)
+        hidden_on_scalar(0, 2)
+        turn(6, 8, "xt0")
+        widen(12, 15)
+        scale_x(2, 4)
+        scale_x(4, 6)
+        quantize_x(2, 4)
+        hidden_on_scalar(2, 4)
+        turn(8, 10, "xt1")
+        scale_x(6, 7)
+        quantize_x(4, 6)
+        hidden_on_scalar(4, 6)
+        turn(10, 12, "acc1")
+        widen(15, 16)
+        interleave(0, 2, 4, 0, 256, G)
+        scale_x(7, 8, 6)
+        turn(12, 14, "xt0")
+        scale_x(8, 10)
+        quantize_x(6, 8)
+        quantize_h(0, 2, 4)
+        hidden_on_scalar(6, 8, into=4)
+        layer2(0, 2, "acc0")
+        turn(14, 16, "xt1")
+        widen(16, 20)
+        interleave(2, 4, 6, 0, 256, G)
+        scale_x(10, 12)
+        add_b2_and_store(0, 2)
+        quantize_x(8, 12)
+        quantize_h(2, 4, 6)
+
+        done = [(2, 4)] + [(4 * u, 4 * u + 4) for u in range(1, 16)]
+        for k in range(3, 15):
+            a = 4 * k
+            cut = {3: G_ROWS - 48, 4: G_ROWS - 96}.get(k, G_ROWS)
+            bank = "acc%d" % (k % 2)
+            interleave(a - 8, a - 4, a - 4, cut, 512, S)
+            interleave(a - 8, a - 4, a - 4, 0, cut, G)
+            if k < 14:
+                hidden_on_scalar(a - 4, a)
             else:
-                quantize_x(s)
-                quantize_h(s - 2)
-        scale_step(last)
-        quantize_x(last)
-        hidden(last)
-        interleave_h(last, "scalar")
-        interleave_h(last - 2, "vector")
-        add_b2_and_store(last - 3)
-        interleave_h(last - 1, "vector")
-        quantize_h(last - 2)
-        layer2(last - 2)
-        quantize_h(last - 1)
-        layer2(last - 1)
-        interleave_h(last, "vector")
-        add_b2_and_store(last - 1)
-        quantize_h(last)
-        layer2(last, "xt0")
-        add_b2_and_store(last - 2)
-        add_b2_and_store(last)
+                hidden_in_halves(a - 4)
+                interleave(a - 4, a - 2, SPARE, 0, 256, S)
+            if k == 3:
+                layer2(*done[0], "acc0")
+            widen(a + 8, a + 12)
+            scale_x(a, a + 2)
+            turn(a + 4, a + 6, "xt0")
+            if k > 3:
+                layer2(*done[k - 3], bank)
+            scale_x(a + 2, a + 4)
+            if k < 14:
+                turn(a + 6, a + 8, "xt1")
+            if k != 4:
+                add_b2_and_store(*done[max(k - 4, 0)])
+            quantize_x(a, a + 4)
+            quantize_h(a - 8, a - 4, a - 4)
+
+        hidden_in_halves(56)
+        turn(62, 64, "xt1")
+        layer2(48, 52, "acc1")
+        interleave(54, 56, 56, 0, 256, G)
+        scale_x(60, 62)
+        add_b2_and_store(44, 48)
+        quantize_x(60, 62)
+        quantize_h(52, 54, SPARE)
+        hidden_on_scalar(60, 62)
+        layer2(52, 54, "xt0")
+        interleave(56, 58, 60, 0, 256, G)
+        interleave(58, 60, 58, 0, 256, S)
+        scale_x(62, 64)
+        add_b2_and_store(48, 52)
+        quantize_x(62, 64)
+        quantize_h(54, 56, 56)
+        quantize_h(56, 58, 60)
+        for t in range(PACK):
+            layer1(62, 64, t, "h%d" % t)
+        layer2(54, 58, "acc0")
+        interleave(60, 62, 56, 0, 256, G)
+        add_b2_and_store(52, 54)
+        for t in range(PACK):
+            relu(62, 64, t, on_vector=t >= 2)
+        add_b2_and_store(54, 58)
+        quantize_h(58, 60, 58)
+        layer2(58, 60, "xt1")
+        interleave(62, 64, 52, 0, 176, S)
+        interleave(62, 64, 52, 176, 256, V)
+        quantize_h(60, 62, 56)
+        layer2(60, 62, "acc1")
+        quantize_h(62, 64, 52)
+        layer2(62, 64, "xt0")
+        add_b2_and_store(58, 60)
+        add_b2_and_store(60, 62)
+        add_b2_and_store(62, 64)

@@ -26,8 +26,8 @@ TILES = ROWS // P
 RING = 12
 SPARE = -2
 H_RING = 16
-LOADS = [2, 4, 6, 6, 6] + [8] * 5
-G_ROWS = 464
+LOADS = [2, 2, 6, 6] + [8] * 6
+G_ROWS = 512
 assert sum(LOADS) == TILES
 
 
@@ -76,11 +76,11 @@ def tile_dpn_t_w4_kernel(tc, x_bytes, x_scale, W1_words, W1_scales, b1, W2_words
         nc.sync.dma_start(out=w1_raw[:], in_=W1_words[0])
         load(1)
         nc.sync.dma_start(out=x_scales[:], in_=x_scale.rearrange("o (p t) -> p (o t)", t=PACK))
+        load(2)
         load_scale_rows(w1s_raw, W1_scales[0].bitcast(I32))
         make_identity(nc, ident[:])
-        load(2)
-        nc.sync.dma_start(out=b1_col[:], in_=b1.rearrange("(p t) -> p t", t=PACK))
         load(3)
+        nc.sync.dma_start(out=b1_col[:], in_=b1.rearrange("(p t) -> p t", t=PACK))
         load(4)
         nc.sync.dma_start(out=w2[:], in_=W2_words.rearrange("g p n -> p g n"))
         load_scale_rows(w2s, W2_scales.bitcast(I32).rearrange("g q n -> q g n"))
@@ -237,8 +237,8 @@ def tile_dpn_t_w4_kernel(tc, x_bytes, x_scale, W1_words, W1_scales, b1, W2_words
         widen(1, 2, copy_by_activation)
         widen(2, 4)
         widen(4, 6)
-        widen(6, 9)
-        widen(9, 12)
+        widen(6, 10)
+        widen(10, 13)
         turn(0, 1, "xt0")
         turn(1, 2, "xt1")
         turn(2, 4, "acc0")
@@ -250,17 +250,17 @@ def tile_dpn_t_w4_kernel(tc, x_bytes, x_scale, W1_words, W1_scales, b1, W2_words
         quantize_x(0, 2)
         hidden_on_scalar(0, 2)
         turn(6, 8, "xt0")
-        widen(12, 15)
+        turn(8, 10, "xt1")
+        widen(13, 17)
         scale_x(2, 4)
         scale_x(4, 6)
         quantize_x(2, 4)
         hidden_on_scalar(2, 4)
-        turn(8, 10, "xt1")
+        turn(10, 12, "acc1")
         scale_x(6, 7)
         quantize_x(4, 6)
         hidden_on_scalar(4, 6)
-        turn(10, 12, "acc1")
-        widen(15, 16)
+        widen(17, 18)
         interleave(0, 2, 4, 0, 256, G)
         scale_x(7, 8, 6)
         turn(12, 14, "xt0")
@@ -270,18 +270,16 @@ def tile_dpn_t_w4_kernel(tc, x_bytes, x_scale, W1_words, W1_scales, b1, W2_words
         hidden_on_scalar(6, 8, into=4)
         layer2(0, 2, "acc0")
         turn(14, 16, "xt1")
-        widen(16, 20)
         interleave(2, 4, 6, 0, 256, G)
+        widen(18, 20)
         scale_x(10, 12)
-        add_b2_and_store(0, 2)
+        scale_x(12, 13)
         quantize_x(8, 12)
         quantize_h(2, 4, 6)
 
-        done = [(2, 4)] + [(4 * u, 4 * u + 4) for u in range(1, 16)]
         for k in range(3, 15):
             a = 4 * k
-            cut = {3: G_ROWS - 48, 4: G_ROWS - 96}.get(k, G_ROWS)
-            bank = "acc%d" % (k % 2)
+            cut = {3: 368, 4: 448}.get(k, G_ROWS)
             interleave(a - 8, a - 4, a - 4, cut, 512, S)
             interleave(a - 8, a - 4, a - 4, 0, cut, G)
             if k < 14:
@@ -290,17 +288,19 @@ def tile_dpn_t_w4_kernel(tc, x_bytes, x_scale, W1_words, W1_scales, b1, W2_words
                 hidden_in_halves(a - 4)
                 interleave(a - 4, a - 2, SPARE, 0, 256, S)
             if k == 3:
-                layer2(*done[0], "acc0")
+                layer2(2, 4, "acc1")
             widen(a + 8, a + 12)
-            scale_x(a, a + 2)
+            scale_x(a + (k == 3), a + 2, a)
             turn(a + 4, a + 6, "xt0")
             if k > 3:
-                layer2(*done[k - 3], bank)
+                layer2(a - 12, a - 8, "acc%d" % (k % 2))
             scale_x(a + 2, a + 4)
             if k < 14:
                 turn(a + 6, a + 8, "xt1")
-            if k != 4:
-                add_b2_and_store(*done[max(k - 4, 0)])
+            if k < 5:
+                add_b2_and_store(2 * k - 6, 2 * k - 4)
+            else:
+                add_b2_and_store(a - 16, a - 12)
             quantize_x(a, a + 4)
             quantize_h(a - 8, a - 4, a - 4)
 

@@ -10,6 +10,7 @@ F32 = mybir.dt.float32
 BF16 = mybir.dt.bfloat16
 U32 = mybir.dt.uint32
 I32 = mybir.dt.int32
+U16 = mybir.dt.uint16
 U8 = mybir.dt.uint8
 FP8 = mybir.dt.float8_e4m3fn
 FP8X4 = mybir.dt.float8_e4m3fn_x4
@@ -25,10 +26,18 @@ PACK = 4
 TILES = ROWS // P
 RING = 12
 SPARE = -2
-H_RING = 16
-LOADS = [2, 2, 6, 6] + [8] * 6
-G_ROWS = 512
+H_RING = 40
+LOADS = [2, 2, 4, 4, 6, 6] + [8] * 5
+G_ROWS = 464
 assert sum(LOADS) == TILES
+LAST = 13
+ADD_TILES = 2
+ADDS = {}
+CUTS = {3: 368}
+EARLY4 = 0
+G15 = 208
+LAST_G = 128
+TURN_AT = 3
 
 
 def tile_dpn_t_w4_kernel(tc, x_bytes, x_scale, W1_words, W1_scales, b1, W2_words, W2_scales, b2, out):
@@ -73,10 +82,10 @@ def tile_dpn_t_w4_kernel(tc, x_bytes, x_scale, W1_words, W1_scales, b1, W2_words
         nc.vector.memset(w1s_raw[:].bitcast(U32), 0)
         nc.vector.memset(w2s[:].rearrange("p g n -> p (g n)").bitcast(U32), 0)
         load(0)
-        nc.sync.dma_start(out=w1_raw[:], in_=W1_words[0])
         load(1)
-        nc.sync.dma_start(out=x_scales[:], in_=x_scale.rearrange("o (p t) -> p (o t)", t=PACK))
         load(2)
+        nc.gpsimd.dma_start(out=w1_raw[:].bitcast(I32), in_=W1_words[0].bitcast(I32))
+        nc.sync.dma_start(out=x_scales[:], in_=x_scale.rearrange("o (p t) -> p (o t)", t=PACK))
         load_scale_rows(w1s_raw, W1_scales[0].bitcast(I32))
         make_identity(nc, ident[:])
         load(3)
@@ -89,9 +98,9 @@ def tile_dpn_t_w4_kernel(tc, x_bytes, x_scale, W1_words, W1_scales, b1, W2_words
             load(i)
 
         def permute_codes():
-            nc.vector.tensor_copy(
-                out=w1[:].rearrange("p (t m b) -> p t m b", t=PACK, b=2),
-                in_=w1_raw[:].rearrange("p (m t b) -> p t m b", t=PACK, b=2),
+            nc.scalar.copy(
+                out=w1[:].bitcast(U16).rearrange("p (t m) -> p t m", t=PACK),
+                in_=w1_raw[:].bitcast(U16).rearrange("p (m t) -> p t m", t=PACK),
             )
 
         def permute_scales():
@@ -123,6 +132,7 @@ def tile_dpn_t_w4_kernel(tc, x_bytes, x_scale, W1_words, W1_scales, b1, W2_words
         def ring(a, b):
             a0 = RING if a == SPARE else a % RING
             return staged[:, D_IN * a0 : D_IN * (a0 + b - a)]
+
 
         def scale_x(a, b, first=None):
             first = a if first is None else first
@@ -231,35 +241,50 @@ def tile_dpn_t_w4_kernel(tc, x_bytes, x_scale, W1_words, W1_scales, b1, W2_words
                 layer1(a, b, t, "h%d" % t)
                 relu(a, b, t, into=into)
 
+        def layer1_pair(a):
+            first = 2 * (a // 2 % 2)
+            for t in range(PACK):
+                layer1(a, a + 2, t, "h%d" % (first + t // 2) if t % 2 == 0 else t - 1)
+
+        def relu_pair(a, into=None):
+            for t in range(PACK):
+                relu(a, a + 2, t, into=into)
+
         S, V, G = nc.scalar, nc.vector, nc.gpsimd
 
         widen(0, 1, nc.vector.tensor_copy)
         widen(1, 2, copy_by_activation)
-        widen(2, 4)
+        widen(2, 3, nc.vector.tensor_copy)
+        widen(3, 4)
         widen(4, 6)
-        widen(6, 10)
-        widen(10, 13)
+        widen(6, 8)
+        permute_codes()
+        widen(8, 12)
         turn(0, 1, "xt0")
         turn(1, 2, "xt1")
-        turn(2, 4, "acc0")
-        turn(4, 6, "acc1")
-        permute_codes()
-        scale_x(0, 1)
-        scale_x(1, 2)
+        turn(2, 4, "acc")
+        turn(4, 6, "back")
         permute_scales()
-        quantize_x(0, 2)
-        hidden_on_scalar(0, 2)
+        scale_x(0, 1)
         turn(6, 8, "xt0")
+        scale_x(1, 2)
+        scale_x(2, 3)
+        quantize_x(0, 2)
+        layer1_pair(0)
+        widen(12, 14)
+        relu_pair(0)
         turn(8, 10, "xt1")
-        widen(13, 17)
-        scale_x(2, 4)
+        scale_x(3, 4, 2)
         scale_x(4, 6)
         quantize_x(2, 4)
-        hidden_on_scalar(2, 4)
-        turn(10, 12, "acc1")
+        layer1_pair(2)
+        widen(14, 17)
+        relu_pair(2)
+        turn(10, 12, "back")
         scale_x(6, 7)
         quantize_x(4, 6)
-        hidden_on_scalar(4, 6)
+        layer1_pair(4)
+        relu_pair(4)
         widen(17, 18)
         interleave(0, 2, 4, 0, 256, G)
         scale_x(7, 8, 6)
@@ -267,76 +292,109 @@ def tile_dpn_t_w4_kernel(tc, x_bytes, x_scale, W1_words, W1_scales, b1, W2_words
         scale_x(8, 10)
         quantize_x(6, 8)
         quantize_h(0, 2, 4)
-        hidden_on_scalar(6, 8, into=4)
-        layer2(0, 2, "acc0")
+        layer1_pair(6)
+        relu_pair(6, into=4)
+        layer2(0, 2, "acc")
         turn(14, 16, "xt1")
         interleave(2, 4, 6, 0, 256, G)
         widen(18, 20)
+        widen(20, 22)
         scale_x(10, 12)
-        scale_x(12, 13)
+        scale_x(12, 14)
+        turn(16, 18, "xt0")
         quantize_x(8, 12)
         quantize_h(2, 4, 6)
 
-        for k in range(3, 15):
+        waiting = (0, 2)
+        wide, done = 22, 2
+
+        def turn_pair(a):
+            turn(a, a + 2, ("xt0", "back", "xt1")[(a // 2 + 1) % 3])
+
+        for k in range(3, LAST + 1):
             a = 4 * k
-            cut = {3: 368, 4: 448}.get(k, G_ROWS)
+            cut = CUTS.get(k, G_ROWS)
             interleave(a - 8, a - 4, a - 4, cut, 512, S)
             interleave(a - 8, a - 4, a - 4, 0, cut, G)
-            if k < 14:
-                hidden_on_scalar(a - 4, a)
-            else:
-                hidden_in_halves(a - 4)
-                interleave(a - 4, a - 2, SPARE, 0, 256, S)
-            if k == 3:
-                layer2(2, 4, "acc1")
-            widen(a + 8, a + 12)
-            scale_x(a + (k == 3), a + 2, a)
-            turn(a + 4, a + 6, "xt0")
-            if k > 3:
-                layer2(a - 12, a - 8, "acc%d" % (k % 2))
+            add_b2_and_store(*waiting)
+            hidden_on_scalar(a - 4, a, (0, 1))
+            turn_pair(a + 6)
+            hidden_on_scalar(a - 4, a, (2, 3))
+            widen(wide, wide + 2)
+            widen(wide + 2, wide + 4)
+            wide = wide + 4
+            waiting = (done, done + ADDS.get(k, ADD_TILES))
+            done = waiting[1]
+            layer2(*waiting, "acc")
             scale_x(a + 2, a + 4)
-            if k < 14:
-                turn(a + 6, a + 8, "xt1")
-            if k < 5:
-                add_b2_and_store(2 * k - 6, 2 * k - 4)
-            else:
-                add_b2_and_store(a - 16, a - 12)
+            turn_pair(a + 8)
+            scale_x(a + 4, a + 6)
             quantize_x(a, a + 4)
             quantize_h(a - 8, a - 4, a - 4)
+        todo = [(j, min(j + 4, 56)) for j in range(done, 56, 4)]
 
-        hidden_in_halves(56)
-        turn(62, 64, "xt1")
-        layer2(48, 52, "acc1")
-        interleave(54, 56, 56, 0, 256, G)
+        def next_layer2(bank):
+            group = todo.pop(0)
+            layer2(*group, bank)
+            return group
+
+        interleave(48, 52, 52, 0, 512, G)
+        add_b2_and_store(*waiting)
+        for t in range(PACK):
+            layer1(52, 56, t, "h%d" % t)
+            relu(52, 54, t)
+            if t == TURN_AT:
+                turn_pair(62)
+        for t in range(PACK):
+            relu(54, 56, t, first=52)
+        interleave(52, 54, SPARE, 0, 256, S)
+        g0 = next_layer2("acc")
+        scale_x(58, 60)
+        g1 = next_layer2("xt0")
         scale_x(60, 62)
-        add_b2_and_store(44, 48)
-        quantize_x(60, 62)
-        quantize_h(52, 54, SPARE)
-        hidden_on_scalar(60, 62)
-        layer2(52, 54, "xt0")
-        interleave(56, 58, 60, 0, 256, G)
-        interleave(58, 60, 58, 0, 256, S)
+        g2 = next_layer2("back")
+        add_b2_and_store(g0[0], g0[0] + 2)
+        quantize_x(56, 60)
+        quantize_h(48, 52, 52)
+        interleave(54, 56, 56, G15, 256, S)
+        interleave(54, 56, 56, 0, G15, G)
+        hidden_on_scalar(56, 60)
         scale_x(62, 64)
-        add_b2_and_store(48, 52)
-        quantize_x(62, 64)
+        g3 = next_layer2("xt1")
+        add_b2_and_store(g0[0] + 2, g0[0] + 4, g0[0])
+        quantize_x(60, 64)
+        quantize_h(52, 54, SPARE)
         quantize_h(54, 56, 56)
-        quantize_h(56, 58, 60)
+        if EARLY4:
+            g4 = next_layer2("acc")
         for t in range(PACK):
-            layer1(62, 64, t, "h%d" % t)
-        layer2(54, 58, "acc0")
-        interleave(60, 62, 56, 0, 256, G)
-        add_b2_and_store(52, 54)
+            layer1(60, 64, t, "h%d" % t)
+        interleave(56, 60, 52, 0, 512, G)
+        if not EARLY4:
+            g4 = next_layer2("acc")
         for t in range(PACK):
-            relu(62, 64, t, on_vector=t >= 2)
-        add_b2_and_store(54, 58)
-        quantize_h(58, 60, 58)
-        layer2(58, 60, "xt1")
-        interleave(62, 64, 52, 0, 176, S)
-        interleave(62, 64, 52, 176, 256, V)
-        quantize_h(60, 62, 56)
-        layer2(60, 62, "acc1")
+            relu(60, 62, t)
+        for t in range(PACK):
+            relu(62, 64, t, first=60)
+        interleave(60, 62, SPARE, 0, 256, S)
+        add_b2_and_store(*g1)
+        g5 = next_layer2("xt0")
+        add_b2_and_store(*g2)
+        g6 = next_layer2("back")
+        add_b2_and_store(*g3)
+        g7 = next_layer2("xt1")
+        add_b2_and_store(*g4)
+        add_b2_and_store(*g5)
+        quantize_h(56, 60, 52)
+        layer2(56, 60, "acc")
+        interleave(62, 64, 52, 0, LAST_G, G)
+        interleave(62, 64, 52, LAST_G, 256, S)
+        add_b2_and_store(*g6)
+        add_b2_and_store(*g7)
+        quantize_h(60, 62, SPARE)
+        layer2(60, 62, "xt0")
         quantize_h(62, 64, 52)
-        layer2(62, 64, "xt0")
-        add_b2_and_store(58, 60)
+        layer2(62, 64, "back")
+        add_b2_and_store(56, 60)
         add_b2_and_store(60, 62)
         add_b2_and_store(62, 64)

@@ -28,16 +28,17 @@ RING = 12
 SPARE = -2
 H_RING = 40
 LOADS = [2, 2, 4, 4, 6, 6] + [8] * 5
-G_ROWS = 464
+G_ROWS = 472
 assert sum(LOADS) == TILES
 LAST = 13
 ADD_TILES = 2
 ADDS = {}
-CUTS = {3: 368}
+CUTS = {}
 EARLY4 = 0
-G15 = 208
-LAST_G = 128
+G15 = 224
+LAST_G = 112
 TURN_AT = 3
+SPLIT_FROM = 4
 
 
 def tile_dpn_t_w4_kernel(tc, x_bytes, x_scale, W1_words, W1_scales, b1, W2_words, W2_scales, b2, out):
@@ -84,10 +85,10 @@ def tile_dpn_t_w4_kernel(tc, x_bytes, x_scale, W1_words, W1_scales, b1, W2_words
         load(0)
         load(1)
         load(2)
-        nc.gpsimd.dma_start(out=w1_raw[:].bitcast(I32), in_=W1_words[0].bitcast(I32))
         nc.sync.dma_start(out=x_scales[:], in_=x_scale.rearrange("o (p t) -> p (o t)", t=PACK))
         load_scale_rows(w1s_raw, W1_scales[0].bitcast(I32))
         make_identity(nc, ident[:])
+        nc.sync.dma_start(out=w1_raw[:], in_=W1_words[0])
         load(3)
         nc.sync.dma_start(out=b1_col[:], in_=b1.rearrange("(p t) -> p t", t=PACK))
         load(4)
@@ -254,8 +255,7 @@ def tile_dpn_t_w4_kernel(tc, x_bytes, x_scale, W1_words, W1_scales, b1, W2_words
 
         widen(0, 1, nc.vector.tensor_copy)
         widen(1, 2, copy_by_activation)
-        widen(2, 3, nc.vector.tensor_copy)
-        widen(3, 4)
+        widen(2, 4, nc.vector.tensor_copy)
         widen(4, 6)
         widen(6, 8)
         permute_codes()
@@ -278,14 +278,13 @@ def tile_dpn_t_w4_kernel(tc, x_bytes, x_scale, W1_words, W1_scales, b1, W2_words
         scale_x(4, 6)
         quantize_x(2, 4)
         layer1_pair(2)
-        widen(14, 17)
+        widen(14, 18)
         relu_pair(2)
         turn(10, 12, "back")
         scale_x(6, 7)
         quantize_x(4, 6)
         layer1_pair(4)
         relu_pair(4)
-        widen(17, 18)
         interleave(0, 2, 4, 0, 256, G)
         scale_x(7, 8, 6)
         turn(12, 14, "xt0")
@@ -317,9 +316,10 @@ def tile_dpn_t_w4_kernel(tc, x_bytes, x_scale, W1_words, W1_scales, b1, W2_words
             interleave(a - 8, a - 4, a - 4, cut, 512, S)
             interleave(a - 8, a - 4, a - 4, 0, cut, G)
             add_b2_and_store(*waiting)
-            hidden_on_scalar(a - 4, a, (0, 1))
+            early = 2 if k >= SPLIT_FROM else 4
+            hidden_on_scalar(a - 4, a, range(early))
             turn_pair(a + 6)
-            hidden_on_scalar(a - 4, a, (2, 3))
+            hidden_on_scalar(a - 4, a, range(early, 4))
             widen(wide, wide + 2)
             widen(wide + 2, wide + 4)
             wide = wide + 4
@@ -334,21 +334,26 @@ def tile_dpn_t_w4_kernel(tc, x_bytes, x_scale, W1_words, W1_scales, b1, W2_words
         todo = [(j, min(j + 4, 56)) for j in range(done, 56, 4)]
 
         def next_layer2(bank):
+            if not todo:
+                return None
             group = todo.pop(0)
             layer2(*group, bank)
             return group
+
+        def add_group(group):
+            if group:
+                add_b2_and_store(*group)
 
         interleave(48, 52, 52, 0, 512, G)
         add_b2_and_store(*waiting)
         for t in range(PACK):
             layer1(52, 56, t, "h%d" % t)
             relu(52, 54, t)
-            if t == TURN_AT:
-                turn_pair(62)
         for t in range(PACK):
             relu(54, 56, t, first=52)
         interleave(52, 54, SPARE, 0, 256, S)
         g0 = next_layer2("acc")
+        turn_pair(62)
         scale_x(58, 60)
         g1 = next_layer2("xt0")
         scale_x(60, 62)
@@ -365,36 +370,32 @@ def tile_dpn_t_w4_kernel(tc, x_bytes, x_scale, W1_words, W1_scales, b1, W2_words
         quantize_x(60, 64)
         quantize_h(52, 54, SPARE)
         quantize_h(54, 56, 56)
-        if EARLY4:
-            g4 = next_layer2("acc")
-        for t in range(PACK):
-            layer1(60, 64, t, "h%d" % t)
+        layer1_pair(60)
         interleave(56, 60, 52, 0, 512, G)
-        if not EARLY4:
-            g4 = next_layer2("acc")
-        for t in range(PACK):
-            relu(60, 62, t)
-        for t in range(PACK):
-            relu(62, 64, t, first=60)
+        g4 = next_layer2("acc")
+        layer1_pair(62)
+        relu_pair(60)
+        relu_pair(62)
         interleave(60, 62, SPARE, 0, 256, S)
-        add_b2_and_store(*g1)
+        add_group(g1)
         g5 = next_layer2("xt0")
-        add_b2_and_store(*g2)
+        add_group(g2)
         g6 = next_layer2("back")
-        add_b2_and_store(*g3)
+        add_group(g3)
         g7 = next_layer2("xt1")
-        add_b2_and_store(*g4)
-        add_b2_and_store(*g5)
+        add_group(g4)
+        add_group(g5)
         quantize_h(56, 60, 52)
         layer2(56, 60, "acc")
         interleave(62, 64, 52, 0, LAST_G, G)
         interleave(62, 64, 52, LAST_G, 256, S)
-        add_b2_and_store(*g6)
-        add_b2_and_store(*g7)
+        add_group(g6)
+        add_group(g7)
         quantize_h(60, 62, SPARE)
         layer2(60, 62, "xt0")
         quantize_h(62, 64, 52)
         layer2(62, 64, "back")
-        add_b2_and_store(56, 60)
+        add_b2_and_store(56, 58)
+        add_b2_and_store(58, 60, 56)
         add_b2_and_store(60, 62)
         add_b2_and_store(62, 64)

@@ -28,7 +28,7 @@ RING = 12
 SPARE = -2
 H_RING = 40
 LOADS = [2, 2, 4, 4, 6, 6] + [8] * 5
-G_ROWS = 472
+G_ROWS = 464
 assert sum(LOADS) == TILES
 LAST = 13
 ADD_TILES = 2
@@ -219,7 +219,10 @@ def tile_dpn_t_w4_kernel(tc, x_bytes, x_scale, W1_words, W1_scales, b1, W2_words
                         stop=(g == 1),
                     )
 
-        def add_b2_and_store(a, b, first=None):
+        def store(a, b):
+            nc.sync.dma_start(out=out_rows[:, OUT * a : OUT * b], in_=result[:, OUT * a : OUT * b])
+
+        def add_b2_and_store(a, b, first=None, store_from=None):
             first = a if first is None else first
             dst = result[:, OUT * a : OUT * b]
             nc.vector.tensor_tensor(
@@ -228,7 +231,8 @@ def tile_dpn_t_w4_kernel(tc, x_bytes, x_scale, W1_words, W1_scales, b1, W2_words
                 in1=b2_row[:].unsqueeze(1).to_broadcast([P, b - a, OUT]),
                 op=ADD,
             )
-            nc.sync.dma_start(out=out_rows[:, OUT * a : OUT * b], in_=dst)
+            if store_from is None or store_from >= 0:
+                store(a if store_from is None else store_from, b)
 
         def hidden_in_halves(a):
             for t in range(PACK):
@@ -340,9 +344,9 @@ def tile_dpn_t_w4_kernel(tc, x_bytes, x_scale, W1_words, W1_scales, b1, W2_words
             layer2(*group, bank)
             return group
 
-        def add_group(group):
+        def add_group(group, store_from=None):
             if group:
-                add_b2_and_store(*group)
+                add_b2_and_store(*group, None, store_from)
 
         interleave(48, 52, 52, 0, 512, G)
         add_b2_and_store(*waiting)
@@ -395,7 +399,6 @@ def tile_dpn_t_w4_kernel(tc, x_bytes, x_scale, W1_words, W1_scales, b1, W2_words
         layer2(60, 62, "xt0")
         quantize_h(62, 64, 52)
         layer2(62, 64, "back")
-        add_b2_and_store(56, 58)
-        add_b2_and_store(58, 60, 56)
-        add_b2_and_store(60, 62)
-        add_b2_and_store(62, 64)
+        add_b2_and_store(56, 60)
+        add_b2_and_store(60, 62, None, -1)
+        add_b2_and_store(62, 64, None, 60)

@@ -27,7 +27,7 @@ TILES = ROWS // P
 RING = 12
 SPARE = -2
 H_RING = 40
-LOADS = [2, 2, 4, 4, 6, 6] + [8] * 5
+LOADS = [2, 2, 4, 4, 4, 8] + [8] * 5
 G_ROWS = 464
 assert sum(LOADS) == TILES
 LAST = 13
@@ -84,18 +84,19 @@ def tile_dpn_t_w4_kernel(tc, x_bytes, x_scale, W1_words, W1_scales, b1, W2_words
         nc.vector.memset(w2s[:].rearrange("p g n -> p (g n)").bitcast(U32), 0)
         load(0)
         load(1)
-        load(2)
         nc.sync.dma_start(out=x_scales[:], in_=x_scale.rearrange("o (p t) -> p (o t)", t=PACK))
+        load(2)
         load_scale_rows(w1s_raw, W1_scales[0].bitcast(I32))
         make_identity(nc, ident[:])
         nc.sync.dma_start(out=w1_raw[:], in_=W1_words[0])
         load(3)
-        nc.sync.dma_start(out=b1_col[:], in_=b1.rearrange("(p t) -> p t", t=PACK))
         load(4)
+        nc.sync.dma_start(out=b1_col[:], in_=b1.rearrange("(p t) -> p t", t=PACK))
+        load(5)
         nc.sync.dma_start(out=w2[:], in_=W2_words.rearrange("g p n -> p g n"))
         load_scale_rows(w2s, W2_scales.bitcast(I32).rearrange("g q n -> q g n"))
         nc.sync.dma_start(out=b2_row[:], in_=b2.partition_broadcast(P))
-        for i in range(5, len(LOADS)):
+        for i in range(6, len(LOADS)):
             load(i)
 
         def permute_codes():
@@ -204,13 +205,15 @@ def tile_dpn_t_w4_kernel(tc, x_bytes, x_scale, W1_words, W1_scales, b1, W2_words
             else:
                 nc.gpsimd.tensor_scalar(out=dst, in0=src, scalar1=1.0, scalar2=0.0, op0=MULT, op1=ADD)
 
-        def layer2(a, b, bank):
-            sums[a] = psum.tile([P, 4, OUT], F32, name=bank)
+        def layer2(a, b, bank, first=None):
+            if first is None:
+                first = a
+                sums[a] = psum.tile([P, 4, OUT], F32, name=bank)
             for j in range(a, b):
                 for g, codes, exps, col in ((0, x_codes, x_exps, j), (1, h_codes, h_exps, j % H_RING)):
                     cols = slice(P * col, P * (col + 1))
                     nc.tensor.matmul_mx(
-                        out=sums[a][:, j - a, :],
+                        out=sums[first][:, j - first, :],
                         lhsT=codes[:, cols].bitcast(FP8X4),
                         lhsT_scale=exps[:, cols],
                         rhs=w2[:, g, :].bitcast(FP4X4),
@@ -259,7 +262,8 @@ def tile_dpn_t_w4_kernel(tc, x_bytes, x_scale, W1_words, W1_scales, b1, W2_words
 
         widen(0, 1, nc.vector.tensor_copy)
         widen(1, 2, copy_by_activation)
-        widen(2, 4, nc.vector.tensor_copy)
+        widen(2, 3, nc.vector.tensor_copy)
+        widen(3, 4)
         widen(4, 6)
         widen(6, 8)
         permute_codes()
@@ -374,9 +378,11 @@ def tile_dpn_t_w4_kernel(tc, x_bytes, x_scale, W1_words, W1_scales, b1, W2_words
         quantize_x(60, 64)
         quantize_h(52, 54, SPARE)
         quantize_h(54, 56, 56)
+        g4 = todo.pop(0)
+        layer2(g4[0], g4[0] + 2, "acc")
         layer1_pair(60)
         interleave(56, 60, 52, 0, 512, G)
-        g4 = next_layer2("acc")
+        layer2(g4[0] + 2, g4[1], "acc", g4[0])
         layer1_pair(62)
         relu_pair(60)
         relu_pair(62)
@@ -387,8 +393,8 @@ def tile_dpn_t_w4_kernel(tc, x_bytes, x_scale, W1_words, W1_scales, b1, W2_words
         g6 = next_layer2("back")
         add_group(g3)
         g7 = next_layer2("xt1")
-        add_group(g4)
-        add_group(g5)
+        add_group(g4, -1)
+        add_group(g5, g4[0])
         quantize_h(56, 60, 52)
         layer2(56, 60, "acc")
         interleave(62, 64, 52, 0, LAST_G, G)

@@ -222,8 +222,8 @@ def tile_dpn_t_w4_kernel(tc, x_bytes, x_scale, W1_words, W1_scales, b1, W2_words
                         stop=(g == 1),
                     )
 
-        def store(a, b):
-            nc.sync.dma_start(out=out_rows[:, OUT * a : OUT * b], in_=result[:, OUT * a : OUT * b])
+        def store(a, b, queue=nc.sync):
+            queue.dma_start(out=out_rows[:, OUT * a : OUT * b], in_=result[:, OUT * a : OUT * b])
 
         def add_b2_and_store(a, b, first=None, store_from=None):
             first = a if first is None else first
@@ -400,11 +400,13 @@ def tile_dpn_t_w4_kernel(tc, x_bytes, x_scale, W1_words, W1_scales, b1, W2_words
         interleave(62, 64, 52, 0, LAST_G, G)
         interleave(62, 64, 52, LAST_G, 256, S)
         add_group(g6)
-        add_group(g7)
+        add_group(g7, -1)
+        store(*g7, nc.scalar)
         quantize_h(60, 62, SPARE)
         layer2(60, 62, "xt0")
         quantize_h(62, 64, 52)
         layer2(62, 64, "back")
         add_b2_and_store(56, 60)
         add_b2_and_store(60, 62, None, -1)
-        add_b2_and_store(62, 64, None, 60)
+        store(60, 62, nc.scalar)
+        add_b2_and_store(62, 64)

@@ -29,6 +29,7 @@ SPARE = -2
 H_RING = 40
 LOADS = [2, 2, 4, 4, 4, 8] + [8] * 5
 G_ROWS = 464
+PLAIN = 3
 assert sum(LOADS) == TILES
 LAST = 13
 ADD_TILES = 2
@@ -111,12 +112,22 @@ def tile_dpn_t_w4_kernel(tc, x_bytes, x_scale, W1_words, W1_scales, b1, W2_words
                 in_=w1s_raw[:].rearrange("p (m t) -> p t m", t=PACK),
             )
 
-        turned, hidden, planes, sums = {}, {}, {}, {}
+        turned, hidden, planes, sums, spans = {}, {}, {}, {}, {}
 
         def widen(a, b, copy=nc.scalar.copy):
-            cols = slice(int(D_IN * a), int(D_IN * min(b, TILES)))
-            if cols.start < cols.stop:
+            b = min(b, TILES)
+            cols = slice(D_IN * a, D_IN * b)
+            if a >= b:
+                return
+            if a < PLAIN:
                 copy(out=xb[:, cols], in_=x8[:, cols].bitcast(FP8))
+                return
+            copy(
+                out=xb[:, cols].rearrange("p (u n e) -> p u n e", u=2, e=2),
+                in_=x8[:, cols].bitcast(FP8).rearrange("p (n u e) -> p u n e", u=2, e=2),
+            )
+            for j in range(a, b):
+                spans[j] = (a, b)
 
         def copy_by_activation(out, in_):
             nc.scalar.activation(out=out, in_=in_, func=COPY)
@@ -129,7 +140,13 @@ def tile_dpn_t_w4_kernel(tc, x_bytes, x_scale, W1_words, W1_scales, b1, W2_words
             for j in range(b - a):
                 w0 = (a + j) * (D_IN // 2)
                 for u in range(2):
-                    nc.tensor.transpose(turned[a][:, u, j, :], words[:, w0 + u : w0 + D_IN // 2 : 2], ident[:])
+                    if a + j < PLAIN:
+                        src = words[:, w0 + u : w0 + D_IN // 2 : 2]
+                    else:
+                        a0, b0 = spans[a + j]
+                        c0 = a0 * (D_IN // 2) + P * (u * (b0 - a0) + a + j - a0)
+                        src = words[:, c0 : c0 + P]
+                    nc.tensor.transpose(turned[a][:, u, j, :], src, ident[:])
 
         def ring(a, b):
             a0 = RING if a == SPARE else a % RING

@@ -28,8 +28,8 @@ RING = 12
 SPARE = -2
 H_RING = 40
 LOADS = [2, 2, 4, 4, 4, 8] + [8] * 5
-G_ROWS = 464
-PLAIN = 3
+G_ROWS = 448
+PLAIN = (1, 3)
 assert sum(LOADS) == TILES
 LAST = 13
 ADD_TILES = 2
@@ -52,6 +52,7 @@ def tile_dpn_t_w4_kernel(tc, x_bytes, x_scale, W1_words, W1_scales, b1, W2_words
         ctx.enter_context(tc.manual_schedule())
 
         ident = keep.tile([P, P], F32, name="ident")
+        ident16 = keep.tile([P, P], BF16, name="ident16")
         x_scales = keep.tile([P, PACK], F32, name="x_scales")
         w1_raw = keep.tile([P, HID * 2], U8, name="w1_raw", align_bytes=64)
         w1 = keep.tile([P, HID * 2], U8, name="w1", align_bytes=64)
@@ -112,14 +113,14 @@ def tile_dpn_t_w4_kernel(tc, x_bytes, x_scale, W1_words, W1_scales, b1, W2_words
                 in_=w1s_raw[:].rearrange("p (m t) -> p t m", t=PACK),
             )
 
-        turned, hidden, planes, sums, spans = {}, {}, {}, {}, {}
+        turned, hidden, planes, sums, spans, woven = {}, {}, {}, {}, {}, {}
 
         def widen(a, b, copy=nc.scalar.copy):
             b = min(b, TILES)
             cols = slice(D_IN * a, D_IN * b)
             if a >= b:
                 return
-            if a < PLAIN:
+            if a in PLAIN:
                 copy(out=xb[:, cols], in_=x8[:, cols].bitcast(FP8))
                 return
             copy(
@@ -129,9 +130,6 @@ def tile_dpn_t_w4_kernel(tc, x_bytes, x_scale, W1_words, W1_scales, b1, W2_words
             for j in range(a, b):
                 spans[j] = (a, b)
 
-        def copy_by_activation(out, in_):
-            nc.scalar.activation(out=out, in_=in_, func=COPY)
-
         def turn(a, b, bank):
             if a >= TILES:
                 return
@@ -140,7 +138,7 @@ def tile_dpn_t_w4_kernel(tc, x_bytes, x_scale, W1_words, W1_scales, b1, W2_words
             for j in range(b - a):
                 w0 = (a + j) * (D_IN // 2)
                 for u in range(2):
-                    if a + j < PLAIN:
+                    if a + j in PLAIN:
                         src = words[:, w0 + u : w0 + D_IN // 2 : 2]
                     else:
                         a0, b0 = spans[a + j]
@@ -222,6 +220,19 @@ def tile_dpn_t_w4_kernel(tc, x_bytes, x_scale, W1_words, W1_scales, b1, W2_words
             else:
                 nc.gpsimd.tensor_scalar(out=dst, in0=src, scalar1=1.0, scalar2=0.0, op0=MULT, op1=ADD)
 
+        def weave(a, r0, r1, bank):
+            woven[a] = psum.tile([P, 8 * P], BF16, name=bank)
+            nc.tensor.matmul(
+                out=woven[a][:, : PACK * (r1 - r0)].rearrange("p (n t) -> p t n", t=PACK),
+                lhsT=ident16[:],
+                rhs=planes[a][:].rearrange("p (t n) -> p t n", t=PACK)[:, :, r0:r1],
+                start=True,
+                stop=True,
+            )
+
+        def take_woven(a, b, slot, r0, r1):
+            nc.scalar.copy(out=ring(slot, slot + b - a)[:, PACK * r0 : PACK * r1], in_=woven[a][:, : PACK * (r1 - r0)])
+
         def layer2(a, b, bank, first=None):
             if first is None:
                 first = a
@@ -254,13 +265,6 @@ def tile_dpn_t_w4_kernel(tc, x_bytes, x_scale, W1_words, W1_scales, b1, W2_words
             if store_from is None or store_from >= 0:
                 store(a if store_from is None else store_from, b)
 
-        def hidden_in_halves(a):
-            for t in range(PACK):
-                layer1(a, a + 4, t, "h%d" % t)
-                relu(a, a + 2, t)
-            for t in range(PACK):
-                relu(a + 2, a + 4, t, first=a)
-
         def hidden_on_scalar(a, b, ts=range(PACK), into=None):
             for t in ts:
                 layer1(a, b, t, "h%d" % t)
@@ -277,10 +281,11 @@ def tile_dpn_t_w4_kernel(tc, x_bytes, x_scale, W1_words, W1_scales, b1, W2_words
 
         S, V, G = nc.scalar, nc.vector, nc.gpsimd
 
-        widen(0, 1, nc.vector.tensor_copy)
-        widen(1, 2, copy_by_activation)
-        widen(2, 3, nc.vector.tensor_copy)
-        widen(3, 4)
+        nc.scalar.activation(out=ident16[:], in_=ident[:], func=COPY)
+        widen(0, 1)
+        widen(1, 2, nc.vector.tensor_copy)
+        widen(2, 3)
+        widen(3, 4, nc.vector.tensor_copy)
         widen(4, 6)
         widen(6, 8)
         permute_codes()
@@ -289,8 +294,8 @@ def tile_dpn_t_w4_kernel(tc, x_bytes, x_scale, W1_words, W1_scales, b1, W2_words
         turn(1, 2, "xt1")
         turn(2, 4, "acc")
         turn(4, 6, "back")
-        permute_scales()
         scale_x(0, 1)
+        permute_scales()
         turn(6, 8, "xt0")
         scale_x(1, 2)
         scale_x(2, 3)
@@ -338,13 +343,18 @@ def tile_dpn_t_w4_kernel(tc, x_bytes, x_scale, W1_words, W1_scales, b1, W2_words
         for k in range(3, LAST + 1):
             a = 4 * k
             cut = CUTS.get(k, G_ROWS)
-            interleave(a - 8, a - 4, a - 4, cut, 512, S)
             interleave(a - 8, a - 4, a - 4, 0, cut, G)
             add_b2_and_store(*waiting)
-            early = 2 if k >= SPLIT_FROM else 4
-            hidden_on_scalar(a - 4, a, range(early))
+            for t in range(2):
+                layer1(a - 4, a, t, "h%d" % ((a + t) % 3))
+            weave(a - 8, cut, 512, "h3")
+            relu(a - 4, a, 0)
+            relu(a - 4, a, 1)
+            take_woven(a - 8, a - 4, a - 4, cut, 512)
             turn_pair(a + 6)
-            hidden_on_scalar(a - 4, a, range(early, 4))
+            for t in range(2, 4):
+                layer1(a - 4, a, t, "h%d" % ((a + t) % 3))
+                relu(a - 4, a, t)
             widen(wide, wide + 2)
             widen(wide + 2, wide + 4)
             wide = wide + 4

@@ -27,16 +27,17 @@ TILES = ROWS // P
 RING = 12
 SPARE = -2
 H_RING = 40
-LOADS = [2, 2, 4, 4, 4, 8] + [8] * 5
+LOADS = [1, 3, 4, 4, 4, 8] + [8] * 5
 G_ROWS = 448
-PLAIN = (1, 3)
+PLAIN = (2, 3, 7, 12, 13)
+IN_RING = (12, 13)
 assert sum(LOADS) == TILES
 LAST = 13
 ADD_TILES = 2
 ADDS = {}
 CUTS = {}
 EARLY4 = 0
-G15 = 224
+G15 = 256
 LAST_G = 112
 TURN_AT = 3
 SPLIT_FROM = 4
@@ -88,9 +89,9 @@ def tile_dpn_t_w4_kernel(tc, x_bytes, x_scale, W1_words, W1_scales, b1, W2_words
         load(1)
         nc.sync.dma_start(out=x_scales[:], in_=x_scale.rearrange("o (p t) -> p (o t)", t=PACK))
         load(2)
-        load_scale_rows(w1s_raw, W1_scales[0].bitcast(I32))
         make_identity(nc, ident[:])
         nc.sync.dma_start(out=w1_raw[:], in_=W1_words[0])
+        load_scale_rows(w1s_raw, W1_scales[0].bitcast(I32))
         load(3)
         load(4)
         nc.sync.dma_start(out=b1_col[:], in_=b1.rearrange("(p t) -> p t", t=PACK))
@@ -108,12 +109,15 @@ def tile_dpn_t_w4_kernel(tc, x_bytes, x_scale, W1_words, W1_scales, b1, W2_words
             )
 
         def permute_scales():
-            nc.vector.tensor_copy(
+            nc.gpsimd.tensor_copy(
                 out=w1s[:].rearrange("p (t m) -> p t m", t=PACK),
                 in_=w1s_raw[:].rearrange("p (m t) -> p t m", t=PACK),
             )
 
         turned, hidden, planes, sums, spans, woven = {}, {}, {}, {}, {}, {}
+
+        def plain_rows(a, b):
+            return ring(a, b) if a in IN_RING else xb[:, D_IN * a : D_IN * b]
 
         def widen(a, b, copy=nc.scalar.copy):
             b = min(b, TILES)
@@ -121,7 +125,7 @@ def tile_dpn_t_w4_kernel(tc, x_bytes, x_scale, W1_words, W1_scales, b1, W2_words
             if a >= b:
                 return
             if a in PLAIN:
-                copy(out=xb[:, cols], in_=x8[:, cols].bitcast(FP8))
+                copy(out=plain_rows(a, b), in_=x8[:, cols].bitcast(FP8))
                 return
             copy(
                 out=xb[:, cols].rearrange("p (u n e) -> p u n e", u=2, e=2),
@@ -136,10 +140,9 @@ def tile_dpn_t_w4_kernel(tc, x_bytes, x_scale, W1_words, W1_scales, b1, W2_words
             words = xb[:].bitcast(F32)
             turned[a] = psum.tile([P, 2, 2, P], F32, name=bank)
             for j in range(b - a):
-                w0 = (a + j) * (D_IN // 2)
                 for u in range(2):
                     if a + j in PLAIN:
-                        src = words[:, w0 + u : w0 + D_IN // 2 : 2]
+                        src = plain_rows(a + j, a + j + 1).bitcast(F32)[:, u : D_IN // 2 : 2]
                     else:
                         a0, b0 = spans[a + j]
                         c0 = a0 * (D_IN // 2) + P * (u * (b0 - a0) + a + j - a0)
@@ -196,7 +199,7 @@ def tile_dpn_t_w4_kernel(tc, x_bytes, x_scale, W1_words, W1_scales, b1, W2_words
             into = a if into is None else into
             n, n0 = P * (b - a), 4 * P * t + P * (a - into)
             if into not in planes:
-                planes[into] = work.tile([P, PACK * 4 * P], BF16, name="planes", bufs=4, align_bytes=64)
+                planes[into] = work.tile([P, PACK * 4 * P], BF16, name="planes", bufs=6, align_bytes=64)
             first = a if first is None else first
             tile, c0 = hidden[first, t]
             c0 = c0 + P * (a - first)
@@ -282,60 +285,66 @@ def tile_dpn_t_w4_kernel(tc, x_bytes, x_scale, W1_words, W1_scales, b1, W2_words
         S, V, G = nc.scalar, nc.vector, nc.gpsimd
 
         nc.scalar.activation(out=ident16[:], in_=ident[:], func=COPY)
-        widen(0, 1)
-        widen(1, 2, nc.vector.tensor_copy)
-        widen(2, 3)
-        widen(3, 4, nc.vector.tensor_copy)
-        widen(4, 6)
-        widen(6, 8)
+        for u in range(2):
+            nc.scalar.copy(
+                out=xb[:, 2 * P * u : 2 * P * (u + 1)].rearrange("p (n e) -> p n e", e=2),
+                in_=x8[:, :D_IN].bitcast(FP8).rearrange("p (n u e) -> p u n e", u=2, e=2)[:, u],
+            )
+        spans[0] = (0, 1)
+        widen(1, 2)
+        widen(2, 4, nc.vector.tensor_copy)
+        widen(4, 7)
+        widen(7, 8, nc.gpsimd.tensor_copy)
+        permute_scales()
         permute_codes()
         widen(8, 12)
         turn(0, 1, "xt0")
         turn(1, 2, "xt1")
-        turn(2, 4, "acc")
+        turn(2, 3, "acc")
+        turn(3, 4, "h2")
         turn(4, 6, "back")
         scale_x(0, 1)
-        permute_scales()
         turn(6, 8, "xt0")
         scale_x(1, 2)
         scale_x(2, 3)
         quantize_x(0, 2)
+        widen(12, 14, nc.gpsimd.tensor_copy)
         layer1_pair(0)
-        widen(12, 14)
+        widen(14, 16)
         relu_pair(0)
         turn(8, 10, "xt1")
-        scale_x(3, 4, 2)
+        scale_x(3, 4)
         scale_x(4, 6)
+        scale_x(6, 7)
         quantize_x(2, 4)
         layer1_pair(2)
-        widen(14, 18)
+        widen(16, 20)
         relu_pair(2)
         turn(10, 12, "back")
-        scale_x(6, 7)
         quantize_x(4, 6)
         layer1_pair(4)
         relu_pair(4)
-        interleave(0, 2, 4, 0, 256, G)
+        interleave(0, 2, 2, 0, 256, G)
         scale_x(7, 8, 6)
         turn(12, 14, "xt0")
         scale_x(8, 10)
+        scale_x(10, 11)
         quantize_x(6, 8)
-        quantize_h(0, 2, 4)
+        quantize_h(0, 2, 2)
         layer1_pair(6)
         relu_pair(6, into=4)
         layer2(0, 2, "acc")
         turn(14, 16, "xt1")
         interleave(2, 4, 6, 0, 256, G)
-        widen(18, 20)
-        widen(20, 22)
-        scale_x(10, 12)
+        widen(20, 24)
+        scale_x(11, 12, 10)
         scale_x(12, 14)
         turn(16, 18, "xt0")
         quantize_x(8, 12)
         quantize_h(2, 4, 6)
 
         waiting = (0, 2)
-        wide, done = 22, 2
+        wide, done = 24, 2
 
         def turn_pair(a):
             turn(a, a + 2, ("xt0", "back", "xt1")[(a // 2 + 1) % 3])
@@ -345,19 +354,20 @@ def tile_dpn_t_w4_kernel(tc, x_bytes, x_scale, W1_words, W1_scales, b1, W2_words
             cut = CUTS.get(k, G_ROWS)
             interleave(a - 8, a - 4, a - 4, 0, cut, G)
             add_b2_and_store(*waiting)
-            for t in range(2):
+            for t in range(3):
                 layer1(a - 4, a, t, "h%d" % ((a + t) % 3))
             weave(a - 8, cut, 512, "h3")
             relu(a - 4, a, 0)
             relu(a - 4, a, 1)
             take_woven(a - 8, a - 4, a - 4, cut, 512)
             turn_pair(a + 6)
-            for t in range(2, 4):
-                layer1(a - 4, a, t, "h%d" % ((a + t) % 3))
-                relu(a - 4, a, t)
+            layer1(a - 4, a, 3, "h%d" % (a % 3))
+            relu(a - 4, a, 2)
+            relu(a - 4, a, 3)
+            ahead = min(TILES, 24 + (62 - 24) * (k - 2) // 10)
             widen(wide, wide + 2)
-            widen(wide + 2, wide + 4)
-            wide = wide + 4
+            widen(wide + 2, ahead)
+            wide = ahead
             waiting = (done, done + ADDS.get(k, ADD_TILES))
             done = waiting[1]
             layer2(*waiting, "acc")
@@ -398,7 +408,11 @@ def tile_dpn_t_w4_kernel(tc, x_bytes, x_scale, W1_words, W1_scales, b1, W2_words
         quantize_h(48, 52, 52)
         interleave(54, 56, 56, G15, 256, S)
         interleave(54, 56, 56, 0, G15, G)
-        hidden_on_scalar(56, 60)
+        for t in range(PACK):
+            layer1(56, 60, t, "h%d" % t)
+            relu(56, 58, t)
+        for t in range(PACK):
+            relu(58, 60, t, first=56)
         scale_x(62, 64)
         g3 = next_layer2("xt1")
         add_b2_and_store(g0[0] + 2, g0[0] + 4, g0[0])
@@ -408,12 +422,15 @@ def tile_dpn_t_w4_kernel(tc, x_bytes, x_scale, W1_words, W1_scales, b1, W2_words
         g4 = todo.pop(0)
         layer2(g4[0], g4[0] + 2, "acc")
         layer1_pair(60)
-        interleave(56, 60, 52, 0, 512, G)
+        interleave(56, 58, SPARE, 0, 256, G)
+        interleave(58, 60, 54, 0, 256, G)
         layer2(g4[0] + 2, g4[1], "acc", g4[0])
         layer1_pair(62)
         relu_pair(60)
         relu_pair(62)
-        interleave(60, 62, SPARE, 0, 256, S)
+        interleave(60, 62, 52, 0, 160, G)
+        interleave(60, 62, 52, 160, 256, S)
+        interleave(62, 64, 56, 0, 256, S)
         add_group(g1)
         g5 = next_layer2("xt0")
         add_group(g2)
@@ -422,16 +439,15 @@ def tile_dpn_t_w4_kernel(tc, x_bytes, x_scale, W1_words, W1_scales, b1, W2_words
         g7 = next_layer2("xt1")
         add_group(g4, -1)
         add_group(g5, g4[0])
-        quantize_h(56, 60, 52)
-        layer2(56, 60, "acc")
-        interleave(62, 64, 52, 0, LAST_G, G)
-        interleave(62, 64, 52, LAST_G, 256, S)
         add_group(g6)
+        quantize_h(56, 58, SPARE)
+        quantize_h(58, 60, 54)
+        layer2(56, 60, "acc")
+        quantize_h(60, 62, 52)
+        layer2(60, 62, "xt0")
         add_group(g7, -1)
         store(*g7, nc.scalar)
-        quantize_h(60, 62, SPARE)
-        layer2(60, 62, "xt0")
-        quantize_h(62, 64, 52)
+        quantize_h(62, 64, 56)
         layer2(62, 64, "back")
         add_b2_and_store(56, 60)
         add_b2_and_store(60, 62, None, -1)

@@ -29,15 +29,15 @@ SPARE = -2
 H_RING = 40
 LOADS = [1, 3, 4, 4, 4, 8] + [8] * 5
 G_ROWS = 448
-PLAIN = (2, 3, 7, 12, 13)
-IN_RING = (12, 13)
+PLAIN = (2, 3, 12)
+IN_RING = (12,)
 assert sum(LOADS) == TILES
 LAST = 13
 ADD_TILES = 2
 ADDS = {}
 CUTS = {}
 EARLY4 = 0
-G15 = 256
+G15 = 224
 LAST_G = 112
 TURN_AT = 3
 SPLIT_FROM = 4
@@ -89,9 +89,9 @@ def tile_dpn_t_w4_kernel(tc, x_bytes, x_scale, W1_words, W1_scales, b1, W2_words
         load(1)
         nc.sync.dma_start(out=x_scales[:], in_=x_scale.rearrange("o (p t) -> p (o t)", t=PACK))
         load(2)
+        load_scale_rows(w1s_raw, W1_scales[0].bitcast(I32))
         make_identity(nc, ident[:])
         nc.sync.dma_start(out=w1_raw[:], in_=W1_words[0])
-        load_scale_rows(w1s_raw, W1_scales[0].bitcast(I32))
         load(3)
         load(4)
         nc.sync.dma_start(out=b1_col[:], in_=b1.rearrange("(p t) -> p t", t=PACK))
@@ -293,8 +293,8 @@ def tile_dpn_t_w4_kernel(tc, x_bytes, x_scale, W1_words, W1_scales, b1, W2_words
         spans[0] = (0, 1)
         widen(1, 2)
         widen(2, 4, nc.vector.tensor_copy)
-        widen(4, 7)
-        widen(7, 8, nc.gpsimd.tensor_copy)
+        widen(4, 6)
+        widen(6, 8)
         permute_scales()
         permute_codes()
         widen(8, 12)
@@ -308,9 +308,9 @@ def tile_dpn_t_w4_kernel(tc, x_bytes, x_scale, W1_words, W1_scales, b1, W2_words
         scale_x(1, 2)
         scale_x(2, 3)
         quantize_x(0, 2)
-        widen(12, 14, nc.gpsimd.tensor_copy)
+        widen(12, 13, nc.gpsimd.tensor_copy)
         layer1_pair(0)
-        widen(14, 16)
+        widen(13, 16)
         relu_pair(0)
         turn(8, 10, "xt1")
         scale_x(3, 4)
@@ -428,8 +428,8 @@ def tile_dpn_t_w4_kernel(tc, x_bytes, x_scale, W1_words, W1_scales, b1, W2_words
         layer1_pair(62)
         relu_pair(60)
         relu_pair(62)
-        interleave(60, 62, 52, 0, 160, G)
-        interleave(60, 62, 52, 160, 256, S)
+        interleave(60, 62, 52, 0, 128, G)
+        interleave(60, 62, 52, 128, 256, S)
         interleave(62, 64, 56, 0, 256, S)
         add_group(g1)
         g5 = next_layer2("xt0")

from contextlib import ExitStack

import concourse.mybir as mybir
from concourse.masks import make_identity

ROWS, D_IN, HID, OUT = 8192, 512, 512, 128
FLOPS = 2 * ROWS * D_IN * HID + 2 * ROWS * (D_IN + HID) * OUT

F32 = mybir.dt.float32
BF16 = mybir.dt.bfloat16
U32 = mybir.dt.uint32
I32 = mybir.dt.int32
U16 = mybir.dt.uint16
U8 = mybir.dt.uint8
FP8 = mybir.dt.float8_e4m3fn
FP8X4 = mybir.dt.float8_e4m3fn_x4
FP4X4 = mybir.dt.float4_e2m1fn_x4
ADD = mybir.AluOpType.add
MULT = mybir.AluOpType.mult
MAX = mybir.AluOpType.max
RELU = mybir.ActivationFunctionType.Relu
COPY = mybir.ActivationFunctionType.Copy

P = 128
PACK = 4
TILES = ROWS // P
RING = 12
SPARE = -2
H_RING = 40
LOADS = [1, 3, 4, 4, 4, 8] + [8] * 5
G_ROWS = 448
PLAIN = (2, 3, 12)
IN_RING = (12,)
assert sum(LOADS) == TILES
LAST = 13
ADD_TILES = 2
ADDS = {}
CUTS = {}
EARLY4 = 0
G15 = 224
LAST_G = 112
TURN_AT = 3
SPLIT_FROM = 4


def tile_dpn_t_w4_kernel(tc, x_bytes, x_scale, W1_words, W1_scales, b1, W2_words, W2_scales, b2, out):
    nc = tc.nc

    with ExitStack() as ctx:
        keep = ctx.enter_context(tc.tile_pool(name="keep", bufs=1))
        work = ctx.enter_context(tc.tile_pool(name="work", bufs=3))
        psum = ctx.enter_context(tc.psum_pool(name="psum", bufs=1))
        ctx.enter_context(tc.manual_schedule())

        ident = keep.tile([P, P], F32, name="ident")
        ident16 = keep.tile([P, P], BF16, name="ident16")
        x_scales = keep.tile([P, PACK], F32, name="x_scales")
        w1_raw = keep.tile([P, HID * 2], U8, name="w1_raw", align_bytes=64)
        w1 = keep.tile([P, HID * 2], U8, name="w1", align_bytes=64)
        w1s_raw = keep.tile([P, HID], U8, name="w1s_raw", align_bytes=64)
        w1s = keep.tile([P, HID], U8, name="w1s", align_bytes=64)
        w2 = keep.tile([P, 2, OUT * 2], U8, name="w2", align_bytes=64)
        w2s = keep.tile([P, 2, OUT], U8, name="w2s", align_bytes=64)
        b1_col = keep.tile([P, PACK], BF16, name="b1_col")
        b2_row = keep.tile([P, OUT], BF16, name="b2_row")
        x8 = keep.tile([P, TILES * D_IN], U8, name="x8", align_bytes=64)
        xb = keep.tile([P, TILES * D_IN], BF16, name="xb", align_bytes=64)
        staged = keep.tile([P, (RING + 2) * D_IN], BF16, name="staged", align_bytes=64)
        x_codes = keep.tile([P, ROWS], U32, name="x_codes", align_bytes=64)
        x_exps = keep.tile([P, ROWS], U8, name="x_exps", align_bytes=64)
        h_codes = keep.tile([P, H_RING * P], U32, name="h_codes", align_bytes=64)
        h_exps = keep.tile([P, H_RING * P], U8, name="h_exps", align_bytes=64)
        result = keep.tile([P, TILES * OUT], F32, name="result")

        x_rows = x_bytes.rearrange("(p j) k -> p (j k)", j=TILES)
        out_rows = out.rearrange("(p j) o -> p (j o)", j=TILES)

        def load(i):
            cols = slice(D_IN * sum(LOADS[:i]), D_IN * sum(LOADS[: i + 1]))
            nc.sync.dma_start(out=x8[:, cols], in_=x_rows[:, cols])

        def load_scale_rows(dst, src):
            for q in range(4):
                nc.sync.dma_start(out=dst[32 * q : 32 * q + 4].bitcast(I32), in_=src[4 * q : 4 * q + 4])

        nc.vector.memset(w1s_raw[:].bitcast(U32), 0)
        nc.vector.memset(w2s[:].rearrange("p g n -> p (g n)").bitcast(U32), 0)
        load(0)
        load(1)
        nc.sync.dma_start(out=x_scales[:], in_=x_scale.rearrange("o (p t) -> p (o t)", t=PACK))
        load(2)
        load_scale_rows(w1s_raw, W1_scales[0].bitcast(I32))
        make_identity(nc, ident[:])
        nc.sync.dma_start(out=w1_raw[:], in_=W1_words[0])
        load(3)
        load(4)
        nc.sync.dma_start(out=b1_col[:], in_=b1.rearrange("(p t) -> p t", t=PACK))
        load(5)
        nc.sync.dma_start(out=w2[:], in_=W2_words.rearrange("g p n -> p g n"))
        load_scale_rows(w2s, W2_scales.bitcast(I32).rearrange("g q n -> q g n"))
        nc.sync.dma_start(out=b2_row[:], in_=b2.partition_broadcast(P))
        for i in range(6, len(LOADS)):
            load(i)

        def permute_codes():
            nc.scalar.copy(
                out=w1[:].bitcast(U16).rearrange("p (t m) -> p t m", t=PACK),
                in_=w1_raw[:].bitcast(U16).rearrange("p (m t) -> p t m", t=PACK),
            )

        def permute_scales():
            nc.gpsimd.tensor_copy(
                out=w1s[:].rearrange("p (t m) -> p t m", t=PACK),
                in_=w1s_raw[:].rearrange("p (m t) -> p t m", t=PACK),
            )

        turned, hidden, planes, sums, spans, woven = {}, {}, {}, {}, {}, {}

        def plain_rows(a, b):
            return ring(a, b) if a in IN_RING else xb[:, D_IN * a : D_IN * b]

        def widen(a, b, copy=nc.scalar.copy):
            b = min(b, TILES)
            cols = slice(D_IN * a, D_IN * b)
            if a >= b:
                return
            if a in PLAIN:
                copy(out=plain_rows(a, b), in_=x8[:, cols].bitcast(FP8))
                return
            copy(
                out=xb[:, cols].rearrange("p (u n e) -> p u n e", u=2, e=2),
                in_=x8[:, cols].bitcast(FP8).rearrange("p (n u e) -> p u n e", u=2, e=2),
            )
            for j in range(a, b):
                spans[j] = (a, b)

        def turn(a, b, bank):
            if a >= TILES:
                return
            words = xb[:].bitcast(F32)
            turned[a] = psum.tile([P, 2, 2, P], F32, name=bank)
            for j in range(b - a):
                for u in range(2):
                    if a + j in PLAIN:
                        src = plain_rows(a + j, a + j + 1).bitcast(F32)[:, u : D_IN // 2 : 2]
                    else:
                        a0, b0 = spans[a + j]
                        c0 = a0 * (D_IN // 2) + P * (u * (b0 - a0) + a + j - a0)
                        src = words[:, c0 : c0 + P]
                    nc.tensor.transpose(turned[a][:, u, j, :], src, ident[:])

        def ring(a, b):
            a0 = RING if a == SPARE else a % RING
            return staged[:, D_IN * a0 : D_IN * (a0 + b - a)]


        def scale_x(a, b, first=None):
            first = a if first is None else first
            n, n0 = P * (b - a), P * (a - first)
            nc.vector.tensor_tensor(
                out=ring(a, b).rearrange("p (n u e) -> p n u e", u=2, e=2),
                in0=turned[first][:]
                .rearrange("p u j n -> p (u j n)")
                .bitcast(BF16)
                .rearrange("p (u n e) -> p n u e", u=2, e=2)[:, n0 : n0 + n],
                in1=x_scales[:].rearrange("p (u e) -> p u e", e=2).unsqueeze(1).to_broadcast([P, n, 2, 2]),
                op=MULT,
            )

        def quantize(codes, exps, a, b, src):
            rows = slice(P * a, P * b)
            nc.vector.quantize_mx(out=codes[:, rows].bitcast(FP8X4), scales=exps[:, rows], in_=src)

        def quantize_x(a, b):
            quantize(x_codes, x_exps, a, b, ring(a, b))

        def quantize_h(a, b, slot):
            quantize(h_codes, h_exps, a % H_RING, a % H_RING + b - a, ring(slot, slot + b - a))

        def layer1(a, b, t, bank):
            n = P * (b - a)
            if isinstance(bank, str):
                tile = psum.tile([P, 4 * P], F32, name=bank)
                hidden[a, t] = tile, 0
            else:
                hidden[a, t] = hidden[a, bank][0], hidden[a, bank][1] + n
            tile, c0 = hidden[a, t]
            nc.tensor.matmul_mx(
                out=tile[:, c0 : c0 + n],
                lhsT=w1[:, 2 * P * t : 2 * P * (t + 1)].bitcast(FP4X4),
                lhsT_scale=w1s[:, P * t : P * (t + 1)],
                rhs=x_codes[:, P * a : P * b].bitcast(FP8X4),
                rhs_scale=x_exps[:, P * a : P * b],
                start=True,
                stop=True,
            )

        def relu(a, b, t, on_vector=False, into=None, first=None):
            into = a if into is None else into
            n, n0 = P * (b - a), 4 * P * t + P * (a - into)
            if into not in planes:
                planes[into] = work.tile([P, PACK * 4 * P], BF16, name="planes", bufs=6, align_bytes=64)
            first = a if first is None else first
            tile, c0 = hidden[first, t]
            c0 = c0 + P * (a - first)
            dst, src = planes[into][:, n0 : n0 + n], tile[:, c0 : c0 + n]
            if on_vector:
                nc.vector.tensor_scalar(out=dst, in0=src, scalar1=b1_col[:, t : t + 1], scalar2=0.0, op0=ADD, op1=MAX)
            else:
                nc.scalar.activation(out=dst, in_=src, func=RELU, bias=b1_col[:, t : t + 1])

        def interleave(a, b, slot, r0, r1, engine):
            if r0 >= r1:
                return
            run = 2 if engine is nc.gpsimd else 4
            src = planes[a][:].rearrange("p (t n) -> p t n", t=PACK)[:, :, r0:r1]
            src = src.rearrange("p t (n i) -> p n t i", i=run)
            dst = ring(slot, slot + b - a)[:, PACK * r0 : PACK * r1].rearrange("p (n i t) -> p n t i", i=run, t=PACK)
            if engine is nc.vector:
                nc.vector.tensor_copy(out=dst, in_=src)
            elif engine is nc.scalar:
                nc.scalar.copy(out=dst, in_=src)
            else:
                nc.gpsimd.tensor_scalar(out=dst, in0=src, scalar1=1.0, scalar2=0.0, op0=MULT, op1=ADD)

        def weave(a, r0, r1, bank):
            woven[a] = psum.tile([P, 8 * P], BF16, name=bank)
            nc.tensor.matmul(
                out=woven[a][:, : PACK * (r1 - r0)].rearrange("p (n t) -> p t n", t=PACK),
                lhsT=ident16[:],
                rhs=planes[a][:].rearrange("p (t n) -> p t n", t=PACK)[:, :, r0:r1],
                start=True,
                stop=True,
            )

        def take_woven(a, b, slot, r0, r1):
            nc.scalar.copy(out=ring(slot, slot + b - a)[:, PACK * r0 : PACK * r1], in_=woven[a][:, : PACK * (r1 - r0)])

        def layer2(a, b, bank, first=None):
            if first is None:
                first = a
                sums[a] = psum.tile([P, 4, OUT], F32, name=bank)
            for j in range(a, b):
                for g, codes, exps, col in ((0, x_codes, x_exps, j), (1, h_codes, h_exps, j % H_RING)):
                    cols = slice(P * col, P * (col + 1))
                    nc.tensor.matmul_mx(
                        out=sums[first][:, j - first, :],
                        lhsT=codes[:, cols].bitcast(FP8X4),
                        lhsT_scale=exps[:, cols],
                        rhs=w2[:, g, :].bitcast(FP4X4),
                        rhs_scale=w2s[:, g, :],
                        start=(g == 0),
                        stop=(g == 1),
                    )

        def store(a, b, queue=nc.sync):
            queue.dma_start(out=out_rows[:, OUT * a : OUT * b], in_=result[:, OUT * a : OUT * b])

        def add_b2_and_store(a, b, first=None, store_from=None):
            first = a if first is None else first
            dst = result[:, OUT * a : OUT * b]
            nc.vector.tensor_tensor(
                out=dst.rearrange("p (j o) -> p j o", o=OUT),
                in0=sums[first][:, a - first : b - first, :],
                in1=b2_row[:].unsqueeze(1).to_broadcast([P, b - a, OUT]),
                op=ADD,
            )
            if store_from is None or store_from >= 0:
                store(a if store_from is None else store_from, b)

        def hidden_on_scalar(a, b, ts=range(PACK), into=None):
            for t in ts:
                layer1(a, b, t, "h%d" % t)
                relu(a, b, t, into=into)

        def layer1_pair(a):
            first = 2 * (a // 2 % 2)
            for t in range(PACK):
                layer1(a, a + 2, t, "h%d" % (first + t // 2) if t % 2 == 0 else t - 1)

        def relu_pair(a, into=None):
            for t in range(PACK):
                relu(a, a + 2, t, into=into)

        S, V, G = nc.scalar, nc.vector, nc.gpsimd

        nc.scalar.activation(out=ident16[:], in_=ident[:], func=COPY)
        for u in range(2):
            nc.scalar.copy(
                out=xb[:, 2 * P * u : 2 * P * (u + 1)].rearrange("p (n e) -> p n e", e=2),
                in_=x8[:, :D_IN].bitcast(FP8).rearrange("p (n u e) -> p u n e", u=2, e=2)[:, u],
            )
        spans[0] = (0, 1)
        widen(1, 2)
        widen(2, 4, nc.vector.tensor_copy)
        widen(4, 6)
        widen(6, 8)
        permute_scales()
        permute_codes()
        widen(8, 12)
        turn(0, 1, "xt0")
        turn(1, 2, "xt1")
        turn(2, 3, "acc")
        turn(3, 4, "h2")
        turn(4, 6, "back")
        scale_x(0, 1)
        turn(6, 8, "xt0")
        scale_x(1, 2)
        scale_x(2, 3)
        quantize_x(0, 2)
        widen(12, 13, nc.gpsimd.tensor_copy)
        layer1_pair(0)
        widen(13, 16)
        relu_pair(0)
        turn(8, 10, "xt1")
        scale_x(3, 4)
        scale_x(4, 6)
        scale_x(6, 7)
        quantize_x(2, 4)
        layer1_pair(2)
        widen(16, 20)
        relu_pair(2)
        turn(10, 12, "back")
        quantize_x(4, 6)
        layer1_pair(4)
        relu_pair(4)
        interleave(0, 2, 2, 0, 256, G)
        scale_x(7, 8, 6)
        turn(12, 14, "xt0")
        scale_x(8, 10)
        scale_x(10, 11)
        quantize_x(6, 8)
        quantize_h(0, 2, 2)
        layer1_pair(6)
        relu_pair(6, into=4)
        layer2(0, 2, "acc")
        turn(14, 16, "xt1")
        interleave(2, 4, 6, 0, 256, G)
        widen(20, 24)
        scale_x(11, 12, 10)
        scale_x(12, 14)
        turn(16, 18, "xt0")
        quantize_x(8, 12)
        quantize_h(2, 4, 6)

        waiting = (0, 2)
        wide, done = 24, 2

        def turn_pair(a):
            turn(a, a + 2, ("xt0", "back", "xt1")[(a // 2 + 1) % 3])

        for k in range(3, LAST + 1):
            a = 4 * k
            cut = CUTS.get(k, G_ROWS)
            interleave(a - 8, a - 4, a - 4, 0, cut, G)
            add_b2_and_store(*waiting)
            for t in range(3):
                layer1(a - 4, a, t, "h%d" % ((a + t) % 3))
            weave(a - 8, cut, 512, "h3")
            relu(a - 4, a, 0)
            relu(a - 4, a, 1)
            take_woven(a - 8, a - 4, a - 4, cut, 512)
            turn_pair(a + 6)
            layer1(a - 4, a, 3, "h%d" % (a % 3))
            relu(a - 4, a, 2)
            relu(a - 4, a, 3)
            ahead = min(TILES, 24 + (62 - 24) * (k - 2) // 10)
            widen(wide, wide + 2)
            widen(wide + 2, ahead)
            wide = ahead
            waiting = (done, done + ADDS.get(k, ADD_TILES))
            done = waiting[1]
            layer2(*waiting, "acc")
            scale_x(a + 2, a + 4)
            turn_pair(a + 8)
            scale_x(a + 4, a + 6)
            quantize_x(a, a + 4)
            quantize_h(a - 8, a - 4, a - 4)
        todo = [(j, min(j + 4, 56)) for j in range(done, 56, 4)]

        def next_layer2(bank):
            if not todo:
                return None
            group = todo.pop(0)
            layer2(*group, bank)
            return group

        def add_group(group, store_from=None):
            if group:
                add_b2_and_store(*group, None, store_from)

        interleave(48, 52, 52, 0, 512, G)
        add_b2_and_store(*waiting)
        for t in range(PACK):
            layer1(52, 56, t, "h%d" % t)
            relu(52, 54, t)
        for t in range(PACK):
            relu(54, 56, t, first=52)
        interleave(52, 54, SPARE, 0, 256, S)
        g0 = next_layer2("acc")
        turn_pair(62)
        scale_x(58, 60)
        g1 = next_layer2("xt0")
        scale_x(60, 62)
        g2 = next_layer2("back")
        add_b2_and_store(g0[0], g0[0] + 2)
        quantize_x(56, 60)
        quantize_h(48, 52, 52)
        interleave(54, 56, 56, G15, 256, S)
        interleave(54, 56, 56, 0, G15, G)
        for t in range(PACK):
            layer1(56, 60, t, "h%d" % t)
            relu(56, 58, t)
        for t in range(PACK):
            relu(58, 60, t, first=56)
        scale_x(62, 64)
        g3 = next_layer2("xt1")
        add_b2_and_store(g0[0] + 2, g0[0] + 4, g0[0])
        quantize_x(60, 64)
        quantize_h(52, 54, SPARE)
        quantize_h(54, 56, 56)
        g4 = todo.pop(0)
        layer2(g4[0], g4[0] + 2, "acc")
        layer1_pair(60)
        interleave(56, 58, SPARE, 0, 256, G)
        interleave(58, 60, 54, 0, 256, G)
        layer2(g4[0] + 2, g4[1], "acc", g4[0])
        layer1_pair(62)
        relu_pair(60)
        relu_pair(62)
        interleave(60, 62, 52, 0, 128, G)
        interleave(60, 62, 52, 128, 256, S)
        interleave(62, 64, 56, 0, 256, S)
        add_group(g1)
        g5 = next_layer2("xt0")
        add_group(g2)
        g6 = next_layer2("back")
        add_group(g3)
        g7 = next_layer2("xt1")
        add_group(g4, -1)
        add_group(g5, g4[0])
        add_group(g6)
        quantize_h(56, 58, SPARE)
        quantize_h(58, 60, 54)
        layer2(56, 60, "acc")
        quantize_h(60, 62, 52)
        layer2(60, 62, "xt0")
        add_group(g7, -1)
        store(*g7, nc.scalar)
        quantize_h(62, 64, 56)
        layer2(62, 64, "back")
        add_b2_and_store(56, 60)
        add_b2_and_store(60, 62, None, -1)
        store(60, 62, nc.scalar)
        add_b2_and_store(62, 64)
